import numpy as np
import ml_dtypes


def mxq(x, axis, fmt="e4m3"):
    dtype, down = {"e4m3": (ml_dtypes.float8_e4m3fn, 7), "e5m2": (ml_dtypes.float8_e5m2, 14)}[fmt]
    v = np.moveaxis(np.asarray(x, np.float32).astype(ml_dtypes.bfloat16).astype(np.float64), axis, -1)
    blocks = v.reshape(v.shape[:-1] + (-1, 32))
    amax = np.abs(blocks).max(-1, keepdims=True)
    byte = np.maximum(np.where(amax > 0, np.frexp(amax)[1] - 1 + 127, 0) - down, 1)
    scale = np.exp2(byte - 127.0)
    codes = (blocks / scale).astype(np.float32).astype(dtype).astype(np.float64)
    return np.moveaxis((codes * scale).reshape(v.shape), -1, axis)


WIDE = False


def mx_kscale(k):
    if not WIDE:
        return np.ones(k)
    levels = np.array([10, -10, 5, -5, 0])
    a = np.random.permutation(np.resize(levels, k // 512 * 4)).reshape(k // 512, 4)
    idx = np.arange(k)
    return np.exp2(a[idx // 512, idx % 128 // 32])


BF16 = ml_dtypes.bfloat16


def bf(x):
    return np.asarray(x, np.float32).astype(BF16)


def f64(x):
    return np.asarray(x).astype(np.float64)


P, N, Z, H1, H2, C = 8, 128, 16, 512, 8192, 128
EPS = 1e-5


def batch_norm(h, gamma, beta):
    mu = h.mean(axis=1, keepdims=True)
    var = h.var(axis=1, keepdims=True)
    return (h - mu) * (1.0 / np.sqrt(var + EPS)) * gamma[:, None, :] + beta[:, None, :]


def setup_inputs():
    r = np.random.standard_normal
    t = mx_kscale(H2)
    sd = np.where(np.random.random((P, 1, H2)) < 0.25, np.sqrt(EPS), 1.0)
    return {"h7_pre": bf((r((P, N, H2)) + 0.5 * r((P, 1, H2))) * sd),
            "g7": bf((1.0 + 0.1 * r((P, H2))) * t),
            "be7": bf(0.3 * r((P, H2)) * t),
            "W8": bf(1.5 * r((P, C, H2)) / np.sqrt(H2) / t),
            "b8": bf(0.5 * r((P, C)))}


def reference(h7_pre, g7, be7, W8, b8):
    a = np.maximum(batch_norm(f64(h7_pre), f64(g7), f64(be7)), 0.0)
    y = (mxq(a, 2, "e4m3") @ mxq(f64(W8), 2, "e4m3").transpose(0, 2, 1)) + f64(b8)[:, None, :]
    em = 1.0 / (1.0 + np.exp(-y))
    return em.transpose(1, 0, 2)

@@ -1,0 +1,165 @@
+from contextlib import ExitStack
+
+import concourse.mybir as mybir
+from concourse.masks import make_identity
+
+F32 = mybir.dt.float32
+BF16 = mybir.dt.bfloat16
+U32 = mybir.dt.uint32
+U8 = mybir.dt.uint8
+FP8X4 = mybir.dt.float8_e4m3fn_x4
+ACT = mybir.ActivationFunctionType
+
+P = 128
+BLOCKS = 8
+ROWS = 128
+CHANNELS = 128
+K = 8192
+EPS = 1e-5
+
+PAIR = 2
+PACK = 4
+TILE_K = PAIR * P
+PASS_K = PACK * P
+PASSES = K // PASS_K
+BANK_TILES = 4
+GROUP_K = 2048
+GROUP_TILES = GROUP_K // TILE_K
+GROUP_PASSES = GROUP_K // PASS_K
+GROUP_BANKS = GROUP_TILES // BANK_TILES
+GROUPS = K // GROUP_K
+BLOCK_TILES = K // TILE_K
+STATS = 6
+
+FLOPS = 2 * BLOCKS * ROWS * CHANNELS * K
+
+
+def tile_decoder_pb_k_kernel(tc, h7_pre, g7, be7, W8, b8, out):
+    nc = tc.nc
+    with ExitStack() as ctx:
+        const = ctx.enter_context(tc.tile_pool(name="const", bufs=1))
+        loads = ctx.enter_context(tc.tile_pool(name="loads", bufs=6))
+        small = ctx.enter_context(tc.tile_pool(name="small", bufs=4))
+        work = ctx.enter_context(tc.tile_pool(name="work", bufs=3))
+        quant = ctx.enter_context(tc.tile_pool(name="quant", bufs=2))
+        psum_h = ctx.enter_context(tc.psum_pool(name="psum_h", bufs=4))
+        psum_w = ctx.enter_context(tc.psum_pool(name="psum_w", bufs=3))
+        psum_y = ctx.enter_context(tc.psum_pool(name="psum_y", bufs=1))
+
+        ident = const.tile([P, P], F32)
+        make_identity(nc, ident[:])
+
+        affine_rows = const.tile([P, 4, TILE_K], BF16)
+        for i, vec in enumerate((g7, be7)):
+            nc.scalar.dma_start(
+                out=affine_rows[:, 2 * i : 2 * i + 2, :],
+                in_=vec.rearrange("b (j c) -> (b j) c", c=TILE_K).rearrange("(s r) c -> r s c", s=2),
+            )
+        affine_ps = psum_w.tile([P, BANK_TILES, P], F32, tag="wT")
+        for i in range(4):
+            nc.tensor.transpose(affine_ps[:, i, :], affine_rows[:, i, :].bitcast(F32), ident[:])
+        affine_words = const.tile([P, 4, P], F32)
+        nc.vector.tensor_copy(out=affine_words[:], in_=affine_ps[:])
+        affine = affine_words[:].bitcast(BF16)
+
+        bias = const.tile([P, BLOCKS * CHANNELS], BF16)
+        nc.scalar.dma_start(out=bias[:], in_=b8.rearrange("b c -> (b c)").partition_broadcast(P))
+        y_sb = const.tile([P, BLOCKS, CHANNELS], F32)
+
+        for b in range(BLOCKS):
+            a_codes = quant.tile([P, PASSES, ROWS], U32, align_bytes=64)
+            a_scales = quant.tile([P, PASSES, ROWS], U8, align_bytes=64)
+            w_codes = quant.tile([P, PASSES, CHANNELS], U32, align_bytes=64)
+            w_scales = quant.tile([P, PASSES, CHANNELS], U8, align_bytes=64)
+            y_ps = psum_y.tile([P, CHANNELS], F32)
+
+            for grp in range(GROUPS):
+                k_cols = slice(grp * GROUP_K, (grp + 1) * GROUP_K)
+                passes = slice(grp * GROUP_PASSES, (grp + 1) * GROUP_PASSES)
+                h_sb = loads.tile([P, GROUP_K], BF16)
+                nc.sync.dma_start(out=h_sb[:], in_=h7_pre[b, :, k_cols])
+                w_sb = loads.tile([P, GROUP_K], BF16)
+                nc.sync.dma_start(out=w_sb[:], in_=W8[b, :, k_cols])
+
+                h_words = h_sb[:].bitcast(F32)
+                stats = small.tile([P, GROUP_TILES, STATS], F32)
+                h_banks = []
+                for bank in range(GROUP_BANKS):
+                    hT = psum_h.tile([P, BANK_TILES, ROWS], F32)
+                    h_banks.append(hT)
+                    for i in range(BANK_TILES):
+                        j = bank * BANK_TILES + i
+                        nc.tensor.transpose(hT[:, i, :], h_words[:, j * P : (j + 1) * P], ident[:])
+                    for i in range(BANK_TILES):
+                        j = bank * BANK_TILES + i
+                        nc.vector.bn_stats(out=stats[:, j, :], in_=hT[:, i, :].bitcast(BF16))
+
+                per_k = stats[:].rearrange("p j (e f) -> p (j e) f", f=3)
+                first = ((b % 4) * BLOCK_TILES + grp * GROUP_TILES) * PAIR
+                gain = affine[:, b // 4, first : first + GROUP_TILES * PAIR]
+                beta = affine[:, 2 + b // 4, first : first + GROUP_TILES * PAIR]
+                spread = small.tile([P, GROUP_TILES * PAIR], F32)
+                nc.scalar.activation(out=spread[:], in_=per_k[:, :, 2], func=ACT.Sqrt, bias=EPS, scale=1.0 / ROWS)
+                scale_k = small.tile([P, GROUP_TILES * PAIR], F32)
+                nc.vector.reciprocal(out=scale_k[:], in_=spread[:])
+                nc.vector.tensor_mul(out=scale_k[:], in0=scale_k[:], in1=gain)
+                shift_k = small.tile([P, GROUP_TILES * PAIR], F32)
+                nc.vector.tensor_mul(out=shift_k[:], in0=per_k[:, :, 1], in1=scale_k[:])
+                nc.vector.tensor_sub(out=shift_k[:], in0=beta, in1=shift_k[:])
+
+                a_planes = work.tile([P, GROUP_PASSES, PACK, ROWS], BF16)
+                for j in range(GROUP_TILES):
+                    pairs = h_banks[j // BANK_TILES][:, j % BANK_TILES, :].bitcast(BF16).rearrange("p (n e) -> p n e", e=PAIR)
+                    for e in range(PAIR):
+                        col = j * PAIR + e
+                        nc.scalar.activation(
+                            out=a_planes[:, j // 2, (j % 2) * PAIR + e, :],
+                            in_=pairs[:, :, e],
+                            func=ACT.Relu,
+                            bias=shift_k[:, col : col + 1],
+                            scale=scale_k[:, col : col + 1],
+                        )
+                a_grouped = work.tile([P, GROUP_PASSES, ROWS, PACK], BF16, align_bytes=64)
+                nc.vector.tensor_copy(
+                    out=a_grouped[:].rearrange("p g (c i) t -> p g c t i", i=4),
+                    in_=a_planes[:].rearrange("p g t (c i) -> p g c t i", i=4),
+                )
+                nc.vector.quantize_mx(
+                    out=a_codes[:, passes, :].rearrange("p g n -> p (g n)").bitcast(FP8X4),
+                    scales=a_scales[:, passes, :].rearrange("p g n -> p (g n)"),
+                    in_=a_grouped[:].rearrange("p g n t -> p (g n t)"),
+                )
+
+                w_words = w_sb[:].bitcast(F32)
+                w_grouped = work.tile([P, GROUP_PASSES, CHANNELS, PACK], BF16, align_bytes=64)
+                w_grouped_words = w_grouped[:].bitcast(F32)
+                for bank in range(GROUP_BANKS):
+                    wT = psum_w.tile([P, BANK_TILES, CHANNELS], F32)
+                    for i in range(BANK_TILES):
+                        j = bank * BANK_TILES + i
+                        nc.tensor.transpose(wT[:, i, :], w_words[:, j * P : (j + 1) * P], ident[:])
+                    nc.scalar.copy(
+                        out=w_grouped_words[:, 2 * bank : 2 * bank + 2, :, :],
+                        in_=wT[:].rearrange("p (g u) c -> p g c u", u=2),
+                    )
+                nc.vector.quantize_mx(
+                    out=w_codes[:, passes, :].rearrange("p g c -> p (g c)").bitcast(FP8X4),
+                    scales=w_scales[:, passes, :].rearrange("p g c -> p (g c)"),
+                    in_=w_grouped[:].rearrange("p g c t -> p (g c t)"),
+                )
+
+                for g in range(grp * GROUP_PASSES, (grp + 1) * GROUP_PASSES):
+                    nc.tensor.matmul_mx(
+                        out=y_ps[:],
+                        lhsT=a_codes[:, g, :].bitcast(FP8X4),
+                        lhsT_scale=a_scales[:, g, :],
+                        rhs=w_codes[:, g, :].bitcast(FP8X4),
+                        rhs_scale=w_scales[:, g, :],
+                        start=(g == 0),
+                        stop=(g == PASSES - 1),
+                    )
+
+            nc.vector.tensor_add(out=y_sb[:, b, :], in0=y_ps[:], in1=bias[:, b * CHANNELS : (b + 1) * CHANNELS])
+
+        nc.scalar.activation(out=y_sb[:], in_=y_sb[:], func=ACT.Sigmoid)
+        nc.sync.dma_start(out=out, in_=y_sb[:])

@@ -9,6 +9,7 @@ U32 = mybir.dt.uint32
 U8 = mybir.dt.uint8
 FP8X4 = mybir.dt.float8_e4m3fn_x4
 ACT = mybir.ActivationFunctionType
+ALU = mybir.AluOpType
 
 P = 128
 BLOCKS = 8
@@ -21,15 +22,17 @@ PAIR = 2
 PACK = 4
 TILE_K = PAIR * P
 PASS_K = PACK * P
-PASSES = K // PASS_K
 BANK_TILES = 4
 GROUP_K = 2048
 GROUP_TILES = GROUP_K // TILE_K
 GROUP_PASSES = GROUP_K // PASS_K
 GROUP_BANKS = GROUP_TILES // BANK_TILES
+GROUP_COLS = GROUP_TILES * PAIR
 GROUPS = K // GROUP_K
+TOTAL = BLOCKS * GROUPS
 BLOCK_TILES = K // TILE_K
 STATS = 6
+AHEAD = 3
 
 FLOPS = 2 * BLOCKS * ROWS * CHANNELS * K
 
@@ -37,14 +40,30 @@ FLOPS = 2 * BLOCKS * ROWS * CHANNELS * K
 def tile_decoder_pb_k_kernel(tc, h7_pre, g7, be7, W8, b8, out):
     nc = tc.nc
     with ExitStack() as ctx:
+        ctx.enter_context(tc.manual_schedule())
         const = ctx.enter_context(tc.tile_pool(name="const", bufs=1))
-        loads = ctx.enter_context(tc.tile_pool(name="loads", bufs=6))
-        small = ctx.enter_context(tc.tile_pool(name="small", bufs=4))
+        loads = ctx.enter_context(tc.tile_pool(name="loads", bufs=AHEAD + 2))
+        small = ctx.enter_context(tc.tile_pool(name="small", bufs=3))
         work = ctx.enter_context(tc.tile_pool(name="work", bufs=3))
-        quant = ctx.enter_context(tc.tile_pool(name="quant", bufs=2))
-        psum_h = ctx.enter_context(tc.psum_pool(name="psum_h", bufs=4))
-        psum_w = ctx.enter_context(tc.psum_pool(name="psum_w", bufs=3))
-        psum_y = ctx.enter_context(tc.psum_pool(name="psum_y", bufs=1))
+        quant = ctx.enter_context(tc.tile_pool(name="quant", bufs=4))
+        psum_h = ctx.enter_context(tc.psum_pool(name="psum_h", bufs=2 * GROUP_BANKS))
+        psum_w = ctx.enter_context(tc.psum_pool(name="psum_w", bufs=GROUP_BANKS))
+        psum_y = ctx.enter_context(tc.psum_pool(name="psum_y", bufs=2))
+
+        h_in, w_in, h_banks, w_banks, stats_of, scale_of, shift_of = {}, {}, {}, {}, {}, {}, {}
+        planes_of, a_grouped_of, w_grouped_of, a_mx, w_mx, y_of = {}, {}, {}, {}, {}, {}
+
+        def load(i):
+            if i >= TOTAL:
+                return
+            b, k_cols = i // GROUPS, slice((i % GROUPS) * GROUP_K, (i % GROUPS + 1) * GROUP_K)
+            h_in[i] = loads.tile([P, GROUP_K], BF16, name="h_sb")
+            nc.sync.dma_start(out=h_in[i][:], in_=h7_pre[b, :, k_cols])
+            w_in[i] = loads.tile([P, GROUP_K], BF16, name="w_sb")
+            nc.sync.dma_start(out=w_in[i][:], in_=W8[b, :, k_cols])
+
+        for i in range(AHEAD):
+            load(i)
 
         ident = const.tile([P, P], F32)
         make_identity(nc, ident[:])
@@ -55,111 +74,163 @@ def tile_decoder_pb_k_kernel(tc, h7_pre, g7, be7, W8, b8, out):
                 out=affine_rows[:, 2 * i : 2 * i + 2, :],
                 in_=vec.rearrange("b (j c) -> (b j) c", c=TILE_K).rearrange("(s r) c -> r s c", s=2),
             )
-        affine_ps = psum_w.tile([P, BANK_TILES, P], F32, tag="wT")
+        bias = const.tile([P, BLOCKS * CHANNELS], BF16)
+        nc.scalar.dma_start(out=bias[:], in_=b8.rearrange("b c -> (b c)").partition_broadcast(P))
+        affine_ps = psum_w.tile([P, BANK_TILES, P], F32, name="wT")
         for i in range(4):
             nc.tensor.transpose(affine_ps[:, i, :], affine_rows[:, i, :].bitcast(F32), ident[:])
         affine_words = const.tile([P, 4, P], F32)
         nc.vector.tensor_copy(out=affine_words[:], in_=affine_ps[:])
         affine = affine_words[:].bitcast(BF16)
-
-        bias = const.tile([P, BLOCKS * CHANNELS], BF16)
-        nc.scalar.dma_start(out=bias[:], in_=b8.rearrange("b c -> (b c)").partition_broadcast(P))
         y_sb = const.tile([P, BLOCKS, CHANNELS], F32)
 
-        for b in range(BLOCKS):
-            a_codes = quant.tile([P, PASSES, ROWS], U32, align_bytes=64)
-            a_scales = quant.tile([P, PASSES, ROWS], U8, align_bytes=64)
-            w_codes = quant.tile([P, PASSES, CHANNELS], U32, align_bytes=64)
-            w_scales = quant.tile([P, PASSES, CHANNELS], U8, align_bytes=64)
-            y_ps = psum_y.tile([P, CHANNELS], F32)
+        def transpose_words(src, pool, name):
+            words = src[:].bitcast(F32)
+            banks = []
+            for bank in range(GROUP_BANKS):
+                turned = pool.tile([P, BANK_TILES, P], F32, name=name)
+                for t in range(BANK_TILES):
+                    j = bank * BANK_TILES + t
+                    nc.tensor.transpose(turned[:, t, :], words[:, j * P : (j + 1) * P], ident[:])
+                banks.append(turned)
+            return banks
 
-            for grp in range(GROUPS):
-                k_cols = slice(grp * GROUP_K, (grp + 1) * GROUP_K)
-                passes = slice(grp * GROUP_PASSES, (grp + 1) * GROUP_PASSES)
-                h_sb = loads.tile([P, GROUP_K], BF16)
-                nc.sync.dma_start(out=h_sb[:], in_=h7_pre[b, :, k_cols])
-                w_sb = loads.tile([P, GROUP_K], BF16)
-                nc.sync.dma_start(out=w_sb[:], in_=W8[b, :, k_cols])
+        def transpose_h(i):
+            if i < TOTAL:
+                h_banks[i] = transpose_words(h_in[i], psum_h, "hT")
 
-                h_words = h_sb[:].bitcast(F32)
-                stats = small.tile([P, GROUP_TILES, STATS], F32)
-                h_banks = []
-                for bank in range(GROUP_BANKS):
-                    hT = psum_h.tile([P, BANK_TILES, ROWS], F32)
-                    h_banks.append(hT)
-                    for i in range(BANK_TILES):
-                        j = bank * BANK_TILES + i
-                        nc.tensor.transpose(hT[:, i, :], h_words[:, j * P : (j + 1) * P], ident[:])
-                    for i in range(BANK_TILES):
-                        j = bank * BANK_TILES + i
-                        nc.vector.bn_stats(out=stats[:, j, :], in_=hT[:, i, :].bitcast(BF16))
+        def statistics(i):
+            if i >= TOTAL:
+                return
+            stats_of[i] = small.tile([P, GROUP_TILES, STATS], F32, name="stats")
+            for j in range(GROUP_TILES):
+                nc.vector.bn_stats(out=stats_of[i][:, j, :], in_=h_banks[i][j // BANK_TILES][:, j % BANK_TILES, :].bitcast(BF16))
 
-                per_k = stats[:].rearrange("p j (e f) -> p (j e) f", f=3)
-                first = ((b % 4) * BLOCK_TILES + grp * GROUP_TILES) * PAIR
-                gain = affine[:, b // 4, first : first + GROUP_TILES * PAIR]
-                beta = affine[:, 2 + b // 4, first : first + GROUP_TILES * PAIR]
-                spread = small.tile([P, GROUP_TILES * PAIR], F32)
-                nc.scalar.activation(out=spread[:], in_=per_k[:, :, 2], func=ACT.Sqrt, bias=EPS, scale=1.0 / ROWS)
-                scale_k = small.tile([P, GROUP_TILES * PAIR], F32)
-                nc.vector.reciprocal(out=scale_k[:], in_=spread[:])
-                nc.vector.tensor_mul(out=scale_k[:], in0=scale_k[:], in1=gain)
-                shift_k = small.tile([P, GROUP_TILES * PAIR], F32)
-                nc.vector.tensor_mul(out=shift_k[:], in0=per_k[:, :, 1], in1=scale_k[:])
-                nc.vector.tensor_sub(out=shift_k[:], in0=beta, in1=shift_k[:])
+        def spread(i):
+            if i >= TOTAL:
+                return
+            per_k = stats_of[i][:].rearrange("p j (e f) -> p (j e) f", f=3)
+            scale_of[i] = small.tile([P, GROUP_COLS], F32, name="scale_k")
+            nc.scalar.activation(out=scale_of[i][:], in_=per_k[:, :, 2], func=ACT.Sqrt, bias=EPS, scale=1.0 / ROWS)
 
-                a_planes = work.tile([P, GROUP_PASSES, PACK, ROWS], BF16)
-                for j in range(GROUP_TILES):
-                    pairs = h_banks[j // BANK_TILES][:, j % BANK_TILES, :].bitcast(BF16).rearrange("p (n e) -> p n e", e=PAIR)
-                    for e in range(PAIR):
-                        col = j * PAIR + e
-                        nc.scalar.activation(
-                            out=a_planes[:, j // 2, (j % 2) * PAIR + e, :],
-                            in_=pairs[:, :, e],
-                            func=ACT.Relu,
-                            bias=shift_k[:, col : col + 1],
-                            scale=scale_k[:, col : col + 1],
-                        )
-                a_grouped = work.tile([P, GROUP_PASSES, ROWS, PACK], BF16, align_bytes=64)
-                nc.vector.tensor_copy(
-                    out=a_grouped[:].rearrange("p g (c i) t -> p g c t i", i=4),
-                    in_=a_planes[:].rearrange("p g t (c i) -> p g c t i", i=4),
-                )
-                nc.vector.quantize_mx(
-                    out=a_codes[:, passes, :].rearrange("p g n -> p (g n)").bitcast(FP8X4),
-                    scales=a_scales[:, passes, :].rearrange("p g n -> p (g n)"),
-                    in_=a_grouped[:].rearrange("p g n t -> p (g n t)"),
-                )
+        def scale_and_shift(i):
+            if i >= TOTAL:
+                return
+            b, grp = i // GROUPS, i % GROUPS
+            per_k = stats_of[i][:].rearrange("p j (e f) -> p (j e) f", f=3)
+            first = ((b % 4) * BLOCK_TILES + grp * GROUP_TILES) * PAIR
+            gain = affine[:, b // 4, first : first + GROUP_COLS]
+            beta = affine[:, 2 + b // 4, first : first + GROUP_COLS]
+            scale_k = scale_of[i]
+            nc.vector.reciprocal(out=scale_k[:], in_=scale_k[:])
+            nc.vector.tensor_mul(out=scale_k[:], in0=scale_k[:], in1=gain)
+            shift_of[i] = small.tile([P, GROUP_COLS], F32, name="shift_k")
+            nc.vector.tensor_mul(out=shift_of[i][:], in0=per_k[:, :, 1], in1=scale_k[:])
+            nc.vector.tensor_sub(out=shift_of[i][:], in0=beta, in1=shift_of[i][:])
 
-                w_words = w_sb[:].bitcast(F32)
-                w_grouped = work.tile([P, GROUP_PASSES, CHANNELS, PACK], BF16, align_bytes=64)
-                w_grouped_words = w_grouped[:].bitcast(F32)
-                for bank in range(GROUP_BANKS):
-                    wT = psum_w.tile([P, BANK_TILES, CHANNELS], F32)
-                    for i in range(BANK_TILES):
-                        j = bank * BANK_TILES + i
-                        nc.tensor.transpose(wT[:, i, :], w_words[:, j * P : (j + 1) * P], ident[:])
-                    nc.scalar.copy(
-                        out=w_grouped_words[:, 2 * bank : 2 * bank + 2, :, :],
-                        in_=wT[:].rearrange("p (g u) c -> p g c u", u=2),
-                    )
-                nc.vector.quantize_mx(
-                    out=w_codes[:, passes, :].rearrange("p g c -> p (g c)").bitcast(FP8X4),
-                    scales=w_scales[:, passes, :].rearrange("p g c -> p (g c)"),
-                    in_=w_grouped[:].rearrange("p g c t -> p (g c t)"),
-                )
-
-                for g in range(grp * GROUP_PASSES, (grp + 1) * GROUP_PASSES):
-                    nc.tensor.matmul_mx(
-                        out=y_ps[:],
-                        lhsT=a_codes[:, g, :].bitcast(FP8X4),
-                        lhsT_scale=a_scales[:, g, :],
-                        rhs=w_codes[:, g, :].bitcast(FP8X4),
-                        rhs_scale=w_scales[:, g, :],
-                        start=(g == 0),
-                        stop=(g == PASSES - 1),
+        def norm_relu(i):
+            if not 0 <= i < TOTAL:
+                return
+            planes_of[i] = work.tile([P, GROUP_PASSES, PACK, ROWS], BF16, name="a_planes")
+            for j in range(GROUP_TILES):
+                pairs = h_banks[i][j // BANK_TILES][:, j % BANK_TILES, :].bitcast(BF16).rearrange("p (n e) -> p n e", e=PAIR)
+                for e in range(PAIR):
+                    col = j * PAIR + e
+                    nc.scalar.activation(
+                        out=planes_of[i][:, j // 2, (j % 2) * PAIR + e, :],
+                        in_=pairs[:, :, e],
+                        func=ACT.Relu,
+                        bias=shift_of[i][:, col : col + 1],
+                        scale=scale_of[i][:, col : col + 1],
                     )
 
-            nc.vector.tensor_add(out=y_sb[:, b, :], in0=y_ps[:], in1=bias[:, b * CHANNELS : (b + 1) * CHANNELS])
+        def regroup(i):
+            if not 0 <= i < TOTAL:
+                return
+            a_grouped_of[i] = work.tile([P, GROUP_PASSES, ROWS, PACK], BF16, name="a_grouped", align_bytes=64)
+            for g in range(GROUP_PASSES):
+                nc.gpsimd.tensor_scalar(
+                    out=a_grouped_of[i][:, g, :, :],
+                    in0=planes_of[i][:, g, :, :].rearrange("p t n -> p n t"),
+                    scalar1=1.0,
+                    scalar2=0.0,
+                    op0=ALU.mult,
+                    op1=ALU.add,
+                )
 
-        nc.scalar.activation(out=y_sb[:], in_=y_sb[:], func=ACT.Sigmoid)
-        nc.sync.dma_start(out=out, in_=y_sb[:])
+        def quantise(i, grouped, name):
+            codes = quant.tile([P, GROUP_PASSES, P], U32, name=name + "_codes", align_bytes=64)
+            scales = quant.tile([P, GROUP_PASSES, P], U8, name=name + "_scales", align_bytes=64)
+            nc.vector.quantize_mx(
+                out=codes[:].rearrange("p g n -> p (g n)").bitcast(FP8X4),
+                scales=scales[:].rearrange("p g n -> p (g n)"),
+                in_=grouped[:].rearrange("p g n t -> p (g n t)"),
+            )
+            return codes, scales
+
+        def quantise_a(i):
+            if 0 <= i < TOTAL:
+                a_mx[i] = quantise(i, a_grouped_of[i], "a")
+
+        def transpose_w(i):
+            if i < TOTAL:
+                w_banks[i] = transpose_words(w_in[i], psum_w, "wT")
+
+        def copy_w(i):
+            if i >= TOTAL:
+                return
+            w_grouped_of[i] = work.tile([P, GROUP_PASSES, CHANNELS, PACK], BF16, name="w_grouped", align_bytes=64)
+            grouped_words = w_grouped_of[i][:].bitcast(F32)
+            for bank, wT in enumerate(w_banks[i]):
+                nc.scalar.copy(
+                    out=grouped_words[:, 2 * bank : 2 * bank + 2, :, :],
+                    in_=wT[:].rearrange("p (g u) c -> p g c u", u=2),
+                )
+
+        def quantise_w(i):
+            if 0 <= i < TOTAL:
+                w_mx[i] = quantise(i, w_grouped_of[i], "w")
+
+        def multiply(i):
+            if not 0 <= i < TOTAL:
+                return
+            b, grp = i // GROUPS, i % GROUPS
+            if grp == 0:
+                y_of[b] = psum_y.tile([P, CHANNELS], F32, name="y_ps")
+            for g in range(GROUP_PASSES):
+                nc.tensor.matmul_mx(
+                    out=y_of[b][:],
+                    lhsT=a_mx[i][0][:, g, :].bitcast(FP8X4),
+                    lhsT_scale=a_mx[i][1][:, g, :],
+                    rhs=w_mx[i][0][:, g, :].bitcast(FP8X4),
+                    rhs_scale=w_mx[i][1][:, g, :],
+                    start=(grp == 0 and g == 0),
+                    stop=(grp == GROUPS - 1 and g == GROUP_PASSES - 1),
+                )
+
+        def add_bias(i):
+            if 0 <= i < TOTAL and i % GROUPS == GROUPS - 1:
+                b = i // GROUPS
+                nc.vector.tensor_add(out=y_sb[:, b, :], in0=y_of[b][:], in1=bias[:, b * CHANNELS : (b + 1) * CHANNELS])
+
+        transpose_h(0)
+        for t in range(TOTAL + 4):
+            load(t + AHEAD)
+            transpose_w(t)
+            statistics(t)
+            norm_relu(t - 1)
+            regroup(t - 1)
+            transpose_h(t + 1)
+            spread(t)
+            copy_w(t)
+            quantise_w(t - 1)
+            scale_and_shift(t)
+            quantise_a(t - 2)
+            add_bias(t - 3)
+            multiply(t - 2)
+
+        last = BLOCKS - 1
+        nc.scalar.activation(out=y_sb[:, :last, :], in_=y_sb[:, :last, :], func=ACT.Sigmoid)
+        nc.sync.dma_start(out=out[:, :last, :], in_=y_sb[:, :last, :])
+        nc.scalar.activation(out=y_sb[:, last, :], in_=y_sb[:, last, :], func=ACT.Sigmoid)
+        nc.sync.dma_start(out=out[:, last, :], in_=y_sb[:, last, :])

@@ -9,7 +9,6 @@ U32 = mybir.dt.uint32
 U8 = mybir.dt.uint8
 FP8X4 = mybir.dt.float8_e4m3fn_x4
 ACT = mybir.ActivationFunctionType
-ALU = mybir.AluOpType
 
 P = 128
 BLOCKS = 8
@@ -32,7 +31,7 @@ GROUPS = K // GROUP_K
 TOTAL = BLOCKS * GROUPS
 BLOCK_TILES = K // TILE_K
 STATS = 6
-AHEAD = 3
+AHEAD = 4
 
 FLOPS = 2 * BLOCKS * ROWS * CHANNELS * K
 
@@ -50,7 +49,7 @@ def tile_decoder_pb_k_kernel(tc, h7_pre, g7, be7, W8, b8, out):
         psum_w = ctx.enter_context(tc.psum_pool(name="psum_w", bufs=GROUP_BANKS))
         psum_y = ctx.enter_context(tc.psum_pool(name="psum_y", bufs=2))
 
-        h_in, w_in, h_banks, w_banks, stats_of, scale_of, shift_of = {}, {}, {}, {}, {}, {}, {}
+        h_in, w_in, h_banks, w_banks, stats_of, spread_of, scale_of, shift_of = {}, {}, {}, {}, {}, {}, {}, {}
         planes_of, a_grouped_of, w_grouped_of, a_mx, w_mx, y_of = {}, {}, {}, {}, {}, {}
 
         def load(i):
@@ -84,55 +83,57 @@ def tile_decoder_pb_k_kernel(tc, h7_pre, g7, be7, W8, b8, out):
         affine = affine_words[:].bitcast(BF16)
         y_sb = const.tile([P, BLOCKS, CHANNELS], F32)
 
-        def transpose_words(src, pool, name):
+        def transpose_words(src, bank, pool, name):
             words = src[:].bitcast(F32)
-            banks = []
-            for bank in range(GROUP_BANKS):
-                turned = pool.tile([P, BANK_TILES, P], F32, name=name)
-                for t in range(BANK_TILES):
-                    j = bank * BANK_TILES + t
-                    nc.tensor.transpose(turned[:, t, :], words[:, j * P : (j + 1) * P], ident[:])
-                banks.append(turned)
-            return banks
+            turned = pool.tile([P, BANK_TILES, P], F32, name=name)
+            for t in range(BANK_TILES):
+                j = bank * BANK_TILES + t
+                nc.tensor.transpose(turned[:, t, :], words[:, j * P : (j + 1) * P], ident[:])
+            return turned
 
-        def transpose_h(i):
+        def transpose_h(i, bank):
             if i < TOTAL:
-                h_banks[i] = transpose_words(h_in[i], psum_h, "hT")
+                h_banks[i] = h_banks.get(i, []) + [transpose_words(h_in[i], bank, psum_h, "hT")]
 
-        def statistics(i):
+        def statistics(i, j):
             if i >= TOTAL:
                 return
-            stats_of[i] = small.tile([P, GROUP_TILES, STATS], F32, name="stats")
-            for j in range(GROUP_TILES):
-                nc.vector.bn_stats(out=stats_of[i][:, j, :], in_=h_banks[i][j // BANK_TILES][:, j % BANK_TILES, :].bitcast(BF16))
+            if j == 0:
+                stats_of[i] = small.tile([P, GROUP_TILES, STATS], F32, name="stats")
+            nc.vector.bn_stats(out=stats_of[i][:, j, :], in_=h_banks[i][j // BANK_TILES][:, j % BANK_TILES, :].bitcast(BF16))
 
         def spread(i):
             if i >= TOTAL:
                 return
             per_k = stats_of[i][:].rearrange("p j (e f) -> p (j e) f", f=3)
-            scale_of[i] = small.tile([P, GROUP_COLS], F32, name="scale_k")
-            nc.scalar.activation(out=scale_of[i][:], in_=per_k[:, :, 2], func=ACT.Sqrt, bias=EPS, scale=1.0 / ROWS)
+            spread_of[i] = small.tile([P, GROUP_COLS], F32, name="spread_k")
+            nc.scalar.activation(out=spread_of[i][:], in_=per_k[:, :, 2], func=ACT.Sqrt, bias=EPS, scale=1.0 / ROWS)
 
         def scale_and_shift(i):
             if i >= TOTAL:
-                return
+                return []
             b, grp = i // GROUPS, i % GROUPS
-            per_k = stats_of[i][:].rearrange("p j (e f) -> p (j e) f", f=3)
+            mean = stats_of[i][:].rearrange("p j (e f) -> p (j e) f", f=3)[:, :, 1]
             first = ((b % 4) * BLOCK_TILES + grp * GROUP_TILES) * PAIR
             gain = affine[:, b // 4, first : first + GROUP_COLS]
             beta = affine[:, 2 + b // 4, first : first + GROUP_COLS]
-            scale_k = scale_of[i]
-            nc.vector.reciprocal(out=scale_k[:], in_=scale_k[:])
-            nc.vector.tensor_mul(out=scale_k[:], in0=scale_k[:], in1=gain)
+            inverse = small.tile([P, GROUP_COLS], F32, name="inverse_k")
+            scale_of[i] = small.tile([P, GROUP_COLS], F32, name="scale_k")
+            centre = small.tile([P, GROUP_COLS], F32, name="centre_k")
             shift_of[i] = small.tile([P, GROUP_COLS], F32, name="shift_k")
-            nc.vector.tensor_mul(out=shift_of[i][:], in0=per_k[:, :, 1], in1=scale_k[:])
-            nc.vector.tensor_sub(out=shift_of[i][:], in0=beta, in1=shift_of[i][:])
+            return [
+                lambda: nc.vector.reciprocal(out=inverse[:], in_=spread_of[i][:]),
+                lambda: nc.vector.tensor_mul(out=scale_of[i][:], in0=inverse[:], in1=gain),
+                lambda: nc.vector.tensor_mul(out=centre[:], in0=mean, in1=scale_of[i][:]),
+                lambda: nc.vector.tensor_sub(out=shift_of[i][:], in0=beta, in1=centre[:]),
+            ]
 
-        def norm_relu(i):
-            if not 0 <= i < TOTAL:
+        def norm_relu(i, bank):
+            if i >= TOTAL:
                 return
-            planes_of[i] = work.tile([P, GROUP_PASSES, PACK, ROWS], BF16, name="a_planes")
-            for j in range(GROUP_TILES):
+            if bank == 0:
+                planes_of[i] = work.tile([P, GROUP_PASSES, PACK, ROWS], BF16, name="a_planes")
+            for j in range(bank * BANK_TILES, (bank + 1) * BANK_TILES):
                 pairs = h_banks[i][j // BANK_TILES][:, j % BANK_TILES, :].bitcast(BF16).rearrange("p (n e) -> p n e", e=PAIR)
                 for e in range(PAIR):
                     col = j * PAIR + e
@@ -148,15 +149,10 @@ def tile_decoder_pb_k_kernel(tc, h7_pre, g7, be7, W8, b8, out):
             if not 0 <= i < TOTAL:
                 return
             a_grouped_of[i] = work.tile([P, GROUP_PASSES, ROWS, PACK], BF16, name="a_grouped", align_bytes=64)
-            for g in range(GROUP_PASSES):
-                nc.gpsimd.tensor_scalar(
-                    out=a_grouped_of[i][:, g, :, :],
-                    in0=planes_of[i][:, g, :, :].rearrange("p t n -> p n t"),
-                    scalar1=1.0,
-                    scalar2=0.0,
-                    op0=ALU.mult,
-                    op1=ALU.add,
-                )
+            nc.vector.tensor_copy(
+                out=a_grouped_of[i][:].rearrange("p g (c i) t -> p g c t i", i=4),
+                in_=planes_of[i][:].rearrange("p g t (c i) -> p g c t i", i=4),
+            )
 
         def quantise(i, grouped, name):
             codes = quant.tile([P, GROUP_PASSES, P], U32, name=name + "_codes", align_bytes=64)
@@ -174,7 +170,7 @@ def tile_decoder_pb_k_kernel(tc, h7_pre, g7, be7, W8, b8, out):
 
         def transpose_w(i):
             if i < TOTAL:
-                w_banks[i] = transpose_words(w_in[i], psum_w, "wT")
+                w_banks[i] = [transpose_words(w_in[i], bank, psum_w, "wT") for bank in range(GROUP_BANKS)]
 
         def copy_w(i):
             if i >= TOTAL:
@@ -213,21 +209,35 @@ def tile_decoder_pb_k_kernel(tc, h7_pre, g7, be7, W8, b8, out):
                 b = i // GROUPS
                 nc.vector.tensor_add(out=y_sb[:, b, :], in0=y_of[b][:], in1=bias[:, b * CHANNELS : (b + 1) * CHANNELS])
 
-        transpose_h(0)
-        for t in range(TOTAL + 4):
+        for bank in range(GROUP_BANKS):
+            transpose_h(0, bank)
+        transpose_w(0)
+        for bank in range(GROUP_BANKS):
+            transpose_h(1, bank)
+        for j in range(GROUP_TILES):
+            statistics(0, j)
+        spread(0)
+        copy_w(0)
+
+        for t in range(TOTAL + 3):
             load(t + AHEAD)
-            transpose_w(t)
-            statistics(t)
-            norm_relu(t - 1)
+            transpose_w(t + 1)
+            steps = scale_and_shift(t)
+            for j in range(GROUP_TILES):
+                if j < len(steps):
+                    steps[j]()
+                statistics(t + 1, j)
+            norm_relu(t, 0)
+            transpose_h(t + 2, 0)
+            spread(t + 1)
+            norm_relu(t, 1)
+            transpose_h(t + 2, 1)
+            copy_w(t + 1)
             regroup(t - 1)
-            transpose_h(t + 1)
-            spread(t)
-            copy_w(t)
-            quantise_w(t - 1)
-            scale_and_shift(t)
-            quantise_a(t - 2)
+            quantise_w(t)
             add_bias(t - 3)
-            multiply(t - 2)
+            quantise_a(t - 1)
+            multiply(t - 1)
 
         last = BLOCKS - 1
         nc.scalar.activation(out=y_sb[:, :last, :], in_=y_sb[:, :last, :], func=ACT.Sigmoid)

@@ -9,6 +9,7 @@ U32 = mybir.dt.uint32
 U8 = mybir.dt.uint8
 FP8X4 = mybir.dt.float8_e4m3fn_x4
 ACT = mybir.ActivationFunctionType
+ALU = mybir.AluOpType
 
 P = 128
 BLOCKS = 8
@@ -31,6 +32,7 @@ GROUPS = K // GROUP_K
 TOTAL = BLOCKS * GROUPS
 BLOCK_TILES = K // TILE_K
 STATS = 6
+VECTOR_PASSES = 2
 AHEAD = 4
 
 FLOPS = 2 * BLOCKS * ROWS * CHANNELS * K
@@ -145,13 +147,25 @@ def tile_decoder_pb_k_kernel(tc, h7_pre, g7, be7, W8, b8, out):
                         scale=scale_of[i][:, col : col + 1],
                     )
 
-        def regroup(i):
-            if not 0 <= i < TOTAL:
+        def regroup_late_passes(i):
+            if i >= TOTAL:
                 return
             a_grouped_of[i] = work.tile([P, GROUP_PASSES, ROWS, PACK], BF16, name="a_grouped", align_bytes=64)
+            nc.gpsimd.tensor_scalar(
+                out=a_grouped_of[i][:, VECTOR_PASSES:, :, :],
+                in0=planes_of[i][:, VECTOR_PASSES:, :, :].rearrange("p g t n -> p g n t"),
+                scalar1=1.0,
+                scalar2=0.0,
+                op0=ALU.mult,
+                op1=ALU.add,
+            )
+
+        def regroup_early_passes(i):
+            if not 0 <= i < TOTAL:
+                return
             nc.vector.tensor_copy(
-                out=a_grouped_of[i][:].rearrange("p g (c i) t -> p g c t i", i=4),
-                in_=planes_of[i][:].rearrange("p g t (c i) -> p g c t i", i=4),
+                out=a_grouped_of[i][:, :VECTOR_PASSES, :, :].rearrange("p g (c i) t -> p g c t i", i=4),
+                in_=planes_of[i][:, :VECTOR_PASSES, :, :].rearrange("p g t (c i) -> p g c t i", i=4),
             )
 
         def quantise(i, grouped, name):
@@ -231,9 +245,10 @@ def tile_decoder_pb_k_kernel(tc, h7_pre, g7, be7, W8, b8, out):
             transpose_h(t + 2, 0)
             spread(t + 1)
             norm_relu(t, 1)
+            regroup_late_passes(t)
             transpose_h(t + 2, 1)
             copy_w(t + 1)
-            regroup(t - 1)
+            regroup_early_passes(t - 1)
             quantise_w(t)
             add_bias(t - 3)
             quantise_a(t - 1)

@@ -22,7 +22,9 @@ PAIR = 2
 PACK = 4
 TILE_K = PAIR * P
 PASS_K = PACK * P
+PASS_TILES = PASS_K // TILE_K
 BANK_TILES = 4
+BANK_PASSES = BANK_TILES // PASS_TILES
 GROUP_K = 2048
 GROUP_TILES = GROUP_K // TILE_K
 GROUP_PASSES = GROUP_K // PASS_K
@@ -32,7 +34,6 @@ GROUPS = K // GROUP_K
 TOTAL = BLOCKS * GROUPS
 BLOCK_TILES = K // TILE_K
 STATS = 6
-VECTOR_PASSES = 2
 AHEAD = 4
 
 FLOPS = 2 * BLOCKS * ROWS * CHANNELS * K
@@ -46,6 +47,7 @@ def tile_decoder_pb_k_kernel(tc, h7_pre, g7, be7, W8, b8, out):
         loads = ctx.enter_context(tc.tile_pool(name="loads", bufs=AHEAD + 2))
         small = ctx.enter_context(tc.tile_pool(name="small", bufs=3))
         work = ctx.enter_context(tc.tile_pool(name="work", bufs=3))
+        single = ctx.enter_context(tc.tile_pool(name="single", bufs=1))
         quant = ctx.enter_context(tc.tile_pool(name="quant", bufs=4))
         psum_h = ctx.enter_context(tc.psum_pool(name="psum_h", bufs=2 * GROUP_BANKS))
         psum_w = ctx.enter_context(tc.psum_pool(name="psum_w", bufs=GROUP_BANKS))
@@ -97,12 +99,16 @@ def tile_decoder_pb_k_kernel(tc, h7_pre, g7, be7, W8, b8, out):
             if i < TOTAL:
                 h_banks[i] = h_banks.get(i, []) + [transpose_words(h_in[i], bank, psum_h, "hT")]
 
-        def statistics(i, j):
+        def transpose_w(i):
+            if i < TOTAL:
+                w_banks[i] = [transpose_words(w_in[i], bank, psum_w, "wT") for bank in range(GROUP_BANKS)]
+
+        def statistics(i):
             if i >= TOTAL:
                 return
-            if j == 0:
-                stats_of[i] = small.tile([P, GROUP_TILES, STATS], F32, name="stats")
-            nc.vector.bn_stats(out=stats_of[i][:, j, :], in_=h_banks[i][j // BANK_TILES][:, j % BANK_TILES, :].bitcast(BF16))
+            stats_of[i] = small.tile([P, GROUP_TILES, STATS], F32, name="stats")
+            for j in range(GROUP_TILES):
+                nc.vector.bn_stats(out=stats_of[i][:, j, :], in_=h_banks[i][j // BANK_TILES][:, j % BANK_TILES, :].bitcast(BF16))
 
         def spread(i):
             if i >= TOTAL:
@@ -130,61 +136,44 @@ def tile_decoder_pb_k_kernel(tc, h7_pre, g7, be7, W8, b8, out):
                 lambda: nc.vector.tensor_sub(out=shift_of[i][:], in0=beta, in1=centre[:]),
             ]
 
-        def norm_relu(i, bank):
+        def norm_relu(i, g):
             if i >= TOTAL:
                 return
-            if bank == 0:
+            if g == 0:
                 planes_of[i] = work.tile([P, GROUP_PASSES, PACK, ROWS], BF16, name="a_planes")
-            for j in range(bank * BANK_TILES, (bank + 1) * BANK_TILES):
+            for u in range(PASS_TILES):
+                j = g * PASS_TILES + u
                 pairs = h_banks[i][j // BANK_TILES][:, j % BANK_TILES, :].bitcast(BF16).rearrange("p (n e) -> p n e", e=PAIR)
                 for e in range(PAIR):
                     col = j * PAIR + e
                     nc.scalar.activation(
-                        out=planes_of[i][:, j // 2, (j % 2) * PAIR + e, :],
+                        out=planes_of[i][:, g, u * PAIR + e, :],
                         in_=pairs[:, :, e],
                         func=ACT.Relu,
                         bias=shift_of[i][:, col : col + 1],
                         scale=scale_of[i][:, col : col + 1],
                     )
 
-        def regroup_late_passes(i):
-            if i >= TOTAL:
+        def regroup_second_bank(i):
+            if not 0 <= i < TOTAL:
                 return
-            a_grouped_of[i] = work.tile([P, GROUP_PASSES, ROWS, PACK], BF16, name="a_grouped", align_bytes=64)
+            a_grouped_of[i] = single.tile([P, GROUP_PASSES, ROWS, PACK], BF16, name="a_grouped", align_bytes=64)
             nc.gpsimd.tensor_scalar(
-                out=a_grouped_of[i][:, VECTOR_PASSES:, :, :],
-                in0=planes_of[i][:, VECTOR_PASSES:, :, :].rearrange("p g t n -> p g n t"),
+                out=a_grouped_of[i][:, BANK_PASSES:, :, :],
+                in0=planes_of[i][:, BANK_PASSES:, :, :].rearrange("p g t n -> p g n t"),
                 scalar1=1.0,
                 scalar2=0.0,
                 op0=ALU.mult,
                 op1=ALU.add,
             )
 
-        def regroup_early_passes(i):
+        def regroup_first_bank(i):
             if not 0 <= i < TOTAL:
                 return
             nc.vector.tensor_copy(
-                out=a_grouped_of[i][:, :VECTOR_PASSES, :, :].rearrange("p g (c i) t -> p g c t i", i=4),
-                in_=planes_of[i][:, :VECTOR_PASSES, :, :].rearrange("p g t (c i) -> p g c t i", i=4),
+                out=a_grouped_of[i][:, :BANK_PASSES, :, :].rearrange("p g (c i) t -> p g c t i", i=4),
+                in_=planes_of[i][:, :BANK_PASSES, :, :].rearrange("p g t (c i) -> p g c t i", i=4),
             )
-
-        def quantise(i, grouped, name):
-            codes = quant.tile([P, GROUP_PASSES, P], U32, name=name + "_codes", align_bytes=64)
-            scales = quant.tile([P, GROUP_PASSES, P], U8, name=name + "_scales", align_bytes=64)
-            nc.vector.quantize_mx(
-                out=codes[:].rearrange("p g n -> p (g n)").bitcast(FP8X4),
-                scales=scales[:].rearrange("p g n -> p (g n)"),
-                in_=grouped[:].rearrange("p g n t -> p (g n t)"),
-            )
-            return codes, scales
-
-        def quantise_a(i):
-            if 0 <= i < TOTAL:
-                a_mx[i] = quantise(i, a_grouped_of[i], "a")
-
-        def transpose_w(i):
-            if i < TOTAL:
-                w_banks[i] = [transpose_words(w_in[i], bank, psum_w, "wT") for bank in range(GROUP_BANKS)]
 
         def copy_w(i):
             if i >= TOTAL:
@@ -193,13 +182,25 @@ def tile_decoder_pb_k_kernel(tc, h7_pre, g7, be7, W8, b8, out):
             grouped_words = w_grouped_of[i][:].bitcast(F32)
             for bank, wT in enumerate(w_banks[i]):
                 nc.scalar.copy(
-                    out=grouped_words[:, 2 * bank : 2 * bank + 2, :, :],
-                    in_=wT[:].rearrange("p (g u) c -> p g c u", u=2),
+                    out=grouped_words[:, bank * BANK_PASSES : (bank + 1) * BANK_PASSES, :, :],
+                    in_=wT[:].rearrange("p (g u) c -> p g c u", u=PASS_TILES),
                 )
 
-        def quantise_w(i):
-            if 0 <= i < TOTAL:
-                w_mx[i] = quantise(i, w_grouped_of[i], "w")
+        def quantise(i, bank, grouped_of, mx_of, name):
+            if not 0 <= i < TOTAL:
+                return
+            if bank == 0:
+                mx_of[i] = (
+                    quant.tile([P, GROUP_PASSES, P], U32, name=name + "_codes", align_bytes=64),
+                    quant.tile([P, GROUP_PASSES, P], U8, name=name + "_scales", align_bytes=64),
+                )
+            codes, scales = mx_of[i]
+            passes = slice(bank * BANK_PASSES, (bank + 1) * BANK_PASSES)
+            nc.vector.quantize_mx(
+                out=codes[:, passes, :].rearrange("p g n -> p (g n)").bitcast(FP8X4),
+                scales=scales[:, passes, :].rearrange("p g n -> p (g n)"),
+                in_=grouped_of[i][:, passes, :, :].rearrange("p g n t -> p (g n t)"),
+            )
 
         def multiply(i):
             if not 0 <= i < TOTAL:
@@ -228,30 +229,36 @@ def tile_decoder_pb_k_kernel(tc, h7_pre, g7, be7, W8, b8, out):
         transpose_w(0)
         for bank in range(GROUP_BANKS):
             transpose_h(1, bank)
-        for j in range(GROUP_TILES):
-            statistics(0, j)
+        statistics(0)
         spread(0)
         copy_w(0)
+        for step in scale_and_shift(0):
+            step()
 
         for t in range(TOTAL + 3):
             load(t + AHEAD)
             transpose_w(t + 1)
-            steps = scale_and_shift(t)
-            for j in range(GROUP_TILES):
-                if j < len(steps):
-                    steps[j]()
-                statistics(t + 1, j)
+            regroup_second_bank(t - 1)
+            statistics(t + 1)
             norm_relu(t, 0)
-            transpose_h(t + 2, 0)
-            spread(t + 1)
             norm_relu(t, 1)
-            regroup_late_passes(t)
+            transpose_h(t + 2, 0)
+            norm_relu(t, 2)
+            spread(t + 1)
+            norm_relu(t, 3)
             transpose_h(t + 2, 1)
             copy_w(t + 1)
-            regroup_early_passes(t - 1)
-            quantise_w(t)
+            regroup_first_bank(t - 1)
             add_bias(t - 3)
-            quantise_a(t - 1)
+            steps = scale_and_shift(t + 1)
+            for bank in range(GROUP_BANKS):
+                if steps:
+                    steps[bank]()
+                quantise(t, bank, w_grouped_of, w_mx, "w")
+            for bank in range(GROUP_BANKS):
+                if steps:
+                    steps[GROUP_BANKS + bank]()
+                quantise(t - 1, bank, a_grouped_of, a_mx, "a")
             multiply(t - 1)
 
         last = BLOCKS - 1

@@ -33,6 +33,8 @@ GROUP_COLS = GROUP_TILES * PAIR
 GROUPS = K // GROUP_K
 TOTAL = BLOCKS * GROUPS
 BLOCK_TILES = K // TILE_K
+HALF_BLOCKS = BLOCKS // 2
+VECTOR_PASSES = 1
 STATS = 6
 AHEAD = 4
 
@@ -54,6 +56,7 @@ def tile_decoder_pb_k_kernel(tc, h7_pre, g7, be7, W8, b8, out):
         psum_y = ctx.enter_context(tc.psum_pool(name="psum_y", bufs=2))
 
         h_in, w_in, h_banks, w_banks, stats_of, spread_of, scale_of, shift_of = {}, {}, {}, {}, {}, {}, {}, {}
+        gain_mean_of, inverse_of, centre_of = {}, {}, {}
         planes_of, a_grouped_of, w_grouped_of, a_mx, w_mx, y_of = {}, {}, {}, {}, {}, {}
 
         def load(i):
@@ -72,16 +75,16 @@ def tile_decoder_pb_k_kernel(tc, h7_pre, g7, be7, W8, b8, out):
         make_identity(nc, ident[:])
 
         affine_rows = const.tile([P, 4, TILE_K], BF16)
-        for i, vec in enumerate((g7, be7)):
+        for v, vec in enumerate((g7, be7)):
             nc.scalar.dma_start(
-                out=affine_rows[:, 2 * i : 2 * i + 2, :],
+                out=affine_rows[:, 2 * v : 2 * v + 2, :],
                 in_=vec.rearrange("b (j c) -> (b j) c", c=TILE_K).rearrange("(s r) c -> r s c", s=2),
             )
         bias = const.tile([P, BLOCKS * CHANNELS], BF16)
         nc.scalar.dma_start(out=bias[:], in_=b8.rearrange("b c -> (b c)").partition_broadcast(P))
         affine_ps = psum_w.tile([P, BANK_TILES, P], F32, name="wT")
-        for i in range(4):
-            nc.tensor.transpose(affine_ps[:, i, :], affine_rows[:, i, :].bitcast(F32), ident[:])
+        for s in range(4):
+            nc.tensor.transpose(affine_ps[:, s, :], affine_rows[:, s, :].bitcast(F32), ident[:])
         affine_words = const.tile([P, 4, P], F32)
         nc.vector.tensor_copy(out=affine_words[:], in_=affine_ps[:])
         affine = affine_words[:].bitcast(BF16)
@@ -90,9 +93,9 @@ def tile_decoder_pb_k_kernel(tc, h7_pre, g7, be7, W8, b8, out):
         def transpose_words(src, bank, pool, name):
             words = src[:].bitcast(F32)
             turned = pool.tile([P, BANK_TILES, P], F32, name=name)
-            for t in range(BANK_TILES):
-                j = bank * BANK_TILES + t
-                nc.tensor.transpose(turned[:, t, :], words[:, j * P : (j + 1) * P], ident[:])
+            for s in range(BANK_TILES):
+                j = bank * BANK_TILES + s
+                nc.tensor.transpose(turned[:, s, :], words[:, j * P : (j + 1) * P], ident[:])
             return turned
 
         def transpose_h(i, bank):
@@ -113,36 +116,50 @@ def tile_decoder_pb_k_kernel(tc, h7_pre, g7, be7, W8, b8, out):
         def spread(i):
             if i >= TOTAL:
                 return
-            per_k = stats_of[i][:].rearrange("p j (e f) -> p (j e) f", f=3)
+            sum_of_squares = stats_of[i][:].rearrange("p j (e f) -> p (j e) f", f=3)[:, :, 2]
             spread_of[i] = small.tile([P, GROUP_COLS], F32, name="spread_k")
-            nc.scalar.activation(out=spread_of[i][:], in_=per_k[:, :, 2], func=ACT.Sqrt, bias=EPS, scale=1.0 / ROWS)
+            nc.scalar.activation(out=spread_of[i][:], in_=sum_of_squares, func=ACT.Sqrt, bias=EPS, scale=1.0 / ROWS)
 
-        def scale_and_shift(i):
-            if i >= TOTAL:
-                return []
+        def per_k(i):
             b, grp = i // GROUPS, i % GROUPS
             mean = stats_of[i][:].rearrange("p j (e f) -> p (j e) f", f=3)[:, :, 1]
-            first = ((b % 4) * BLOCK_TILES + grp * GROUP_TILES) * PAIR
-            gain = affine[:, b // 4, first : first + GROUP_COLS]
-            beta = affine[:, 2 + b // 4, first : first + GROUP_COLS]
-            inverse = small.tile([P, GROUP_COLS], F32, name="inverse_k")
-            scale_of[i] = small.tile([P, GROUP_COLS], F32, name="scale_k")
-            centre = small.tile([P, GROUP_COLS], F32, name="centre_k")
-            shift_of[i] = small.tile([P, GROUP_COLS], F32, name="shift_k")
-            return [
-                lambda: nc.vector.reciprocal(out=inverse[:], in_=spread_of[i][:]),
-                lambda: nc.vector.tensor_mul(out=scale_of[i][:], in0=inverse[:], in1=gain),
-                lambda: nc.vector.tensor_mul(out=centre[:], in0=mean, in1=scale_of[i][:]),
-                lambda: nc.vector.tensor_sub(out=shift_of[i][:], in0=beta, in1=centre[:]),
-            ]
+            first = ((b % HALF_BLOCKS) * BLOCK_TILES + grp * GROUP_TILES) * PAIR
+            gain = affine[:, b // HALF_BLOCKS, first : first + GROUP_COLS]
+            beta = affine[:, 2 + b // HALF_BLOCKS, first : first + GROUP_COLS]
+            return mean, gain, beta
 
-        def norm_relu(i, g):
+        def gain_times_mean(i):
+            if i < TOTAL:
+                mean, gain, beta = per_k(i)
+                gain_mean_of[i] = small.tile([P, GROUP_COLS], F32, name="gain_mean_k")
+                nc.vector.tensor_mul(out=gain_mean_of[i][:], in0=mean, in1=gain)
+
+        def invert_spread(i):
+            if i < TOTAL:
+                inverse_of[i] = small.tile([P, GROUP_COLS], F32, name="inverse_k")
+                nc.vector.reciprocal(out=inverse_of[i][:], in_=spread_of[i][:])
+
+        def scale_and_centre(i):
+            if i < TOTAL:
+                mean, gain, beta = per_k(i)
+                scale_of[i] = small.tile([P, GROUP_COLS], F32, name="scale_k")
+                nc.vector.tensor_mul(out=scale_of[i][:], in0=inverse_of[i][:], in1=gain)
+                centre_of[i] = small.tile([P, GROUP_COLS], F32, name="centre_k")
+                nc.vector.tensor_mul(out=centre_of[i][:], in0=inverse_of[i][:], in1=gain_mean_of[i][:])
+
+        def shift(i):
+            if i < TOTAL:
+                mean, gain, beta = per_k(i)
+                shift_of[i] = small.tile([P, GROUP_COLS], F32, name="shift_k")
+                nc.vector.tensor_sub(out=shift_of[i][:], in0=beta, in1=centre_of[i][:])
+
+        def norm_relu(i, bank):
             if i >= TOTAL:
                 return
-            if g == 0:
+            if bank == 0:
                 planes_of[i] = work.tile([P, GROUP_PASSES, PACK, ROWS], BF16, name="a_planes")
-            for u in range(PASS_TILES):
-                j = g * PASS_TILES + u
+            for j in range(bank * BANK_TILES, (bank + 1) * BANK_TILES):
+                g, u = j // PASS_TILES, j % PASS_TILES
                 pairs = h_banks[i][j // BANK_TILES][:, j % BANK_TILES, :].bitcast(BF16).rearrange("p (n e) -> p n e", e=PAIR)
                 for e in range(PAIR):
                     col = j * PAIR + e
@@ -154,25 +171,25 @@ def tile_decoder_pb_k_kernel(tc, h7_pre, g7, be7, W8, b8, out):
                         scale=scale_of[i][:, col : col + 1],
                     )
 
-        def regroup_second_bank(i):
+        def regroup_on_gpsimd(i):
             if not 0 <= i < TOTAL:
                 return
             a_grouped_of[i] = single.tile([P, GROUP_PASSES, ROWS, PACK], BF16, name="a_grouped", align_bytes=64)
             nc.gpsimd.tensor_scalar(
-                out=a_grouped_of[i][:, BANK_PASSES:, :, :],
-                in0=planes_of[i][:, BANK_PASSES:, :, :].rearrange("p g t n -> p g n t"),
+                out=a_grouped_of[i][:, VECTOR_PASSES:, :, :],
+                in0=planes_of[i][:, VECTOR_PASSES:, :, :].rearrange("p g t n -> p g n t"),
                 scalar1=1.0,
                 scalar2=0.0,
                 op0=ALU.mult,
                 op1=ALU.add,
             )
 
-        def regroup_first_bank(i):
+        def regroup_on_vector(i):
             if not 0 <= i < TOTAL:
                 return
             nc.vector.tensor_copy(
-                out=a_grouped_of[i][:, :BANK_PASSES, :, :].rearrange("p g (c i) t -> p g c t i", i=4),
-                in_=planes_of[i][:, :BANK_PASSES, :, :].rearrange("p g t (c i) -> p g c t i", i=4),
+                out=a_grouped_of[i][:, :VECTOR_PASSES, :, :].rearrange("p g (c i) t -> p g c t i", i=4),
+                in_=planes_of[i][:, :VECTOR_PASSES, :, :].rearrange("p g t (c i) -> p g c t i", i=4),
             )
 
         def copy_w(i):
@@ -232,33 +249,32 @@ def tile_decoder_pb_k_kernel(tc, h7_pre, g7, be7, W8, b8, out):
         statistics(0)
         spread(0)
         copy_w(0)
-        for step in scale_and_shift(0):
-            step()
+        gain_times_mean(0)
+        invert_spread(0)
+        scale_and_centre(0)
+        shift(0)
 
         for t in range(TOTAL + 3):
             load(t + AHEAD)
             transpose_w(t + 1)
-            regroup_second_bank(t - 1)
+            regroup_on_gpsimd(t - 1)
             statistics(t + 1)
             norm_relu(t, 0)
-            norm_relu(t, 1)
             transpose_h(t + 2, 0)
-            norm_relu(t, 2)
             spread(t + 1)
-            norm_relu(t, 3)
+            norm_relu(t, 1)
             transpose_h(t + 2, 1)
             copy_w(t + 1)
-            regroup_first_bank(t - 1)
+            regroup_on_vector(t - 1)
             add_bias(t - 3)
-            steps = scale_and_shift(t + 1)
-            for bank in range(GROUP_BANKS):
-                if steps:
-                    steps[bank]()
-                quantise(t, bank, w_grouped_of, w_mx, "w")
-            for bank in range(GROUP_BANKS):
-                if steps:
-                    steps[GROUP_BANKS + bank]()
-                quantise(t - 1, bank, a_grouped_of, a_mx, "a")
+            gain_times_mean(t + 1)
+            quantise(t, 0, w_grouped_of, w_mx, "w")
+            invert_spread(t + 1)
+            quantise(t, 1, w_grouped_of, w_mx, "w")
+            scale_and_centre(t + 1)
+            quantise(t - 1, 0, a_grouped_of, a_mx, "a")
+            shift(t + 1)
+            quantise(t - 1, 1, a_grouped_of, a_mx, "a")
             multiply(t - 1)
 
         last = BLOCKS - 1

@@ -34,7 +34,7 @@ GROUPS = K // GROUP_K
 TOTAL = BLOCKS * GROUPS
 BLOCK_TILES = K // TILE_K
 HALF_BLOCKS = BLOCKS // 2
-VECTOR_PASSES = 1
+SCALAR_PASSES = 1
 STATS = 6
 AHEAD = 4
 
@@ -57,6 +57,7 @@ def tile_decoder_pb_k_kernel(tc, h7_pre, g7, be7, W8, b8, out):
 
         h_in, w_in, h_banks, w_banks, stats_of, spread_of, scale_of, shift_of = {}, {}, {}, {}, {}, {}, {}, {}
         gain_mean_of, inverse_of, centre_of = {}, {}, {}
+        a_first_of = {}
         planes_of, a_grouped_of, w_grouped_of, a_mx, w_mx, y_of = {}, {}, {}, {}, {}, {}
 
         def load(i):
@@ -174,22 +175,23 @@ def tile_decoder_pb_k_kernel(tc, h7_pre, g7, be7, W8, b8, out):
         def regroup_on_gpsimd(i):
             if not 0 <= i < TOTAL:
                 return
-            a_grouped_of[i] = single.tile([P, GROUP_PASSES, ROWS, PACK], BF16, name="a_grouped", align_bytes=64)
+            a_grouped_of[i] = single.tile([P, GROUP_PASSES - SCALAR_PASSES, ROWS, PACK], BF16, name="a_grouped", align_bytes=64)
             nc.gpsimd.tensor_scalar(
-                out=a_grouped_of[i][:, VECTOR_PASSES:, :, :],
-                in0=planes_of[i][:, VECTOR_PASSES:, :, :].rearrange("p g t n -> p g n t"),
+                out=a_grouped_of[i][:],
+                in0=planes_of[i][:, SCALAR_PASSES:, :, :].rearrange("p g t n -> p g n t"),
                 scalar1=1.0,
                 scalar2=0.0,
                 op0=ALU.mult,
                 op1=ALU.add,
             )
 
-        def regroup_on_vector(i):
+        def regroup_on_scalar(i):
             if not 0 <= i < TOTAL:
                 return
-            nc.vector.tensor_copy(
-                out=a_grouped_of[i][:, :VECTOR_PASSES, :, :].rearrange("p g (c i) t -> p g c t i", i=4),
-                in_=planes_of[i][:, :VECTOR_PASSES, :, :].rearrange("p g t (c i) -> p g c t i", i=4),
+            a_first_of[i] = work.tile([P, SCALAR_PASSES, ROWS, PACK], BF16, name="a_first", align_bytes=64)
+            nc.scalar.copy(
+                out=a_first_of[i][:].rearrange("p g (c i) t -> p g c t i", i=4),
+                in_=planes_of[i][:, :SCALAR_PASSES, :, :].rearrange("p g t (c i) -> p g c t i", i=4),
             )
 
         def copy_w(i):
@@ -203,21 +205,31 @@ def tile_decoder_pb_k_kernel(tc, h7_pre, g7, be7, W8, b8, out):
                     in_=wT[:].rearrange("p (g u) c -> p g c u", u=PASS_TILES),
                 )
 
-        def quantise(i, bank, grouped_of, mx_of, name):
-            if not 0 <= i < TOTAL:
-                return
-            if bank == 0:
+        def quantise(i, passes, grouped, mx_of, name):
+            if i not in mx_of:
                 mx_of[i] = (
                     quant.tile([P, GROUP_PASSES, P], U32, name=name + "_codes", align_bytes=64),
                     quant.tile([P, GROUP_PASSES, P], U8, name=name + "_scales", align_bytes=64),
                 )
             codes, scales = mx_of[i]
-            passes = slice(bank * BANK_PASSES, (bank + 1) * BANK_PASSES)
             nc.vector.quantize_mx(
                 out=codes[:, passes, :].rearrange("p g n -> p (g n)").bitcast(FP8X4),
                 scales=scales[:, passes, :].rearrange("p g n -> p (g n)"),
-                in_=grouped_of[i][:, passes, :, :].rearrange("p g n t -> p (g n t)"),
+                in_=grouped.rearrange("p g n t -> p (g n t)"),
             )
+
+        def quantise_w(i, bank):
+            if 0 <= i < TOTAL:
+                passes = slice(bank * BANK_PASSES, (bank + 1) * BANK_PASSES)
+                quantise(i, passes, w_grouped_of[i][:, passes, :, :], w_mx, "w")
+
+        def quantise_a(i, first, last):
+            if 0 <= i < TOTAL:
+                if first < SCALAR_PASSES:
+                    grouped = a_first_of[i][:, first:last, :, :]
+                else:
+                    grouped = a_grouped_of[i][:, first - SCALAR_PASSES : last - SCALAR_PASSES, :, :]
+                quantise(i, slice(first, last), grouped, a_mx, "a")
 
         def multiply(i):
             if not 0 <= i < TOTAL:
@@ -259,22 +271,22 @@ def tile_decoder_pb_k_kernel(tc, h7_pre, g7, be7, W8, b8, out):
             transpose_w(t + 1)
             regroup_on_gpsimd(t - 1)
             statistics(t + 1)
-            norm_relu(t, 0)
-            transpose_h(t + 2, 0)
+            for bank in range(GROUP_BANKS):
+                norm_relu(t, bank)
+                transpose_h(t + 2, bank)
             spread(t + 1)
-            norm_relu(t, 1)
-            transpose_h(t + 2, 1)
             copy_w(t + 1)
-            regroup_on_vector(t - 1)
+            regroup_on_scalar(t)
             add_bias(t - 3)
             gain_times_mean(t + 1)
-            quantise(t, 0, w_grouped_of, w_mx, "w")
+            quantise_w(t, 0)
             invert_spread(t + 1)
-            quantise(t, 1, w_grouped_of, w_mx, "w")
+            quantise_w(t, 1)
             scale_and_centre(t + 1)
-            quantise(t - 1, 0, a_grouped_of, a_mx, "a")
+            quantise_a(t - 1, 0, 1)
+            quantise_a(t - 1, 1, 2)
             shift(t + 1)
-            quantise(t - 1, 1, a_grouped_of, a_mx, "a")
+            quantise_a(t - 1, 2, 4)
             multiply(t - 1)
 
         last = BLOCKS - 1

@@ -34,7 +34,8 @@ GROUPS = K // GROUP_K
 TOTAL = BLOCKS * GROUPS
 BLOCK_TILES = K // TILE_K
 HALF_BLOCKS = BLOCKS // 2
-SCALAR_PASSES = 1
+FIRST_PASSES = 1
+SCALAR_ROWS = 64
 STATS = 6
 AHEAD = 4
 
@@ -55,8 +56,8 @@ def tile_decoder_pb_k_kernel(tc, h7_pre, g7, be7, W8, b8, out):
         psum_w = ctx.enter_context(tc.psum_pool(name="psum_w", bufs=GROUP_BANKS))
         psum_y = ctx.enter_context(tc.psum_pool(name="psum_y", bufs=2))
 
-        h_in, w_in, h_banks, w_banks, stats_of, spread_of, scale_of, shift_of = {}, {}, {}, {}, {}, {}, {}, {}
-        gain_mean_of, inverse_of, centre_of = {}, {}, {}
+        h_in, w_in, h_banks, w_banks, stats_of, scale_of, shift_of = {}, {}, {}, {}, {}, {}, {}
+        inverse_of, centre_of = {}, {}
         a_first_of = {}
         planes_of, a_grouped_of, w_grouped_of, a_mx, w_mx, y_of = {}, {}, {}, {}, {}, {}
 
@@ -114,12 +115,12 @@ def tile_decoder_pb_k_kernel(tc, h7_pre, g7, be7, W8, b8, out):
             for j in range(GROUP_TILES):
                 nc.vector.bn_stats(out=stats_of[i][:, j, :], in_=h_banks[i][j // BANK_TILES][:, j % BANK_TILES, :].bitcast(BF16))
 
-        def spread(i):
+        def invert_spread(i):
             if i >= TOTAL:
                 return
             sum_of_squares = stats_of[i][:].rearrange("p j (e f) -> p (j e) f", f=3)[:, :, 2]
-            spread_of[i] = small.tile([P, GROUP_COLS], F32, name="spread_k")
-            nc.scalar.activation(out=spread_of[i][:], in_=sum_of_squares, func=ACT.Sqrt, bias=EPS, scale=1.0 / ROWS)
+            inverse_of[i] = small.tile([P, GROUP_COLS], F32, name="inverse_k")
+            nc.scalar.activation(out=inverse_of[i][:], in_=sum_of_squares, func=ACT.Abs_reciprocal_sqrt, bias=EPS, scale=1.0 / ROWS)
 
         def per_k(i):
             b, grp = i // GROUPS, i % GROUPS
@@ -129,24 +130,17 @@ def tile_decoder_pb_k_kernel(tc, h7_pre, g7, be7, W8, b8, out):
             beta = affine[:, 2 + b // HALF_BLOCKS, first : first + GROUP_COLS]
             return mean, gain, beta
 
-        def gain_times_mean(i):
-            if i < TOTAL:
-                mean, gain, beta = per_k(i)
-                gain_mean_of[i] = small.tile([P, GROUP_COLS], F32, name="gain_mean_k")
-                nc.vector.tensor_mul(out=gain_mean_of[i][:], in0=mean, in1=gain)
-
-        def invert_spread(i):
-            if i < TOTAL:
-                inverse_of[i] = small.tile([P, GROUP_COLS], F32, name="inverse_k")
-                nc.vector.reciprocal(out=inverse_of[i][:], in_=spread_of[i][:])
-
-        def scale_and_centre(i):
+        def scale(i):
             if i < TOTAL:
                 mean, gain, beta = per_k(i)
                 scale_of[i] = small.tile([P, GROUP_COLS], F32, name="scale_k")
                 nc.vector.tensor_mul(out=scale_of[i][:], in0=inverse_of[i][:], in1=gain)
+
+        def centre(i):
+            if i < TOTAL:
+                mean, gain, beta = per_k(i)
                 centre_of[i] = small.tile([P, GROUP_COLS], F32, name="centre_k")
-                nc.vector.tensor_mul(out=centre_of[i][:], in0=inverse_of[i][:], in1=gain_mean_of[i][:])
+                nc.vector.tensor_mul(out=centre_of[i][:], in0=mean, in1=scale_of[i][:])
 
         def shift(i):
             if i < TOTAL:
@@ -175,35 +169,36 @@ def tile_decoder_pb_k_kernel(tc, h7_pre, g7, be7, W8, b8, out):
         def regroup_on_gpsimd(i):
             if not 0 <= i < TOTAL:
                 return
-            a_grouped_of[i] = single.tile([P, GROUP_PASSES - SCALAR_PASSES, ROWS, PACK], BF16, name="a_grouped", align_bytes=64)
+            a_grouped_of[i] = single.tile([P, GROUP_PASSES - FIRST_PASSES, ROWS, PACK], BF16, name="a_grouped", align_bytes=64)
             nc.gpsimd.tensor_scalar(
                 out=a_grouped_of[i][:],
-                in0=planes_of[i][:, SCALAR_PASSES:, :, :].rearrange("p g t n -> p g n t"),
+                in0=planes_of[i][:, FIRST_PASSES:, :, :].rearrange("p g t n -> p g n t"),
                 scalar1=1.0,
                 scalar2=0.0,
                 op0=ALU.mult,
                 op1=ALU.add,
             )
 
-        def regroup_on_scalar(i):
+        def regroup_first(i, copy, rows):
             if not 0 <= i < TOTAL:
                 return
-            a_first_of[i] = work.tile([P, SCALAR_PASSES, ROWS, PACK], BF16, name="a_first", align_bytes=64)
-            nc.scalar.copy(
-                out=a_first_of[i][:].rearrange("p g (c i) t -> p g c t i", i=4),
-                in_=planes_of[i][:, :SCALAR_PASSES, :, :].rearrange("p g t (c i) -> p g c t i", i=4),
+            if i not in a_first_of:
+                a_first_of[i] = work.tile([P, FIRST_PASSES, ROWS, PACK], BF16, name="a_first", align_bytes=64)
+            copy(
+                out=a_first_of[i][:, :, rows, :].rearrange("p g (c i) t -> p g c t i", i=4),
+                in_=planes_of[i][:, :FIRST_PASSES, :, rows].rearrange("p g t (c i) -> p g c t i", i=4),
             )
 
-        def copy_w(i):
+        def copy_w(i, bank):
             if i >= TOTAL:
                 return
-            w_grouped_of[i] = work.tile([P, GROUP_PASSES, CHANNELS, PACK], BF16, name="w_grouped", align_bytes=64)
+            if bank == 0:
+                w_grouped_of[i] = work.tile([P, GROUP_PASSES, CHANNELS, PACK], BF16, name="w_grouped", align_bytes=64)
             grouped_words = w_grouped_of[i][:].bitcast(F32)
-            for bank, wT in enumerate(w_banks[i]):
-                nc.scalar.copy(
-                    out=grouped_words[:, bank * BANK_PASSES : (bank + 1) * BANK_PASSES, :, :],
-                    in_=wT[:].rearrange("p (g u) c -> p g c u", u=PASS_TILES),
-                )
+            nc.scalar.copy(
+                out=grouped_words[:, bank * BANK_PASSES : (bank + 1) * BANK_PASSES, :, :],
+                in_=w_banks[i][bank][:].rearrange("p (g u) c -> p g c u", u=PASS_TILES),
+            )
 
         def quantise(i, passes, grouped, mx_of, name):
             if i not in mx_of:
@@ -225,10 +220,10 @@ def tile_decoder_pb_k_kernel(tc, h7_pre, g7, be7, W8, b8, out):
 
         def quantise_a(i, first, last):
             if 0 <= i < TOTAL:
-                if first < SCALAR_PASSES:
+                if first < FIRST_PASSES:
                     grouped = a_first_of[i][:, first:last, :, :]
                 else:
-                    grouped = a_grouped_of[i][:, first - SCALAR_PASSES : last - SCALAR_PASSES, :, :]
+                    grouped = a_grouped_of[i][:, first - FIRST_PASSES : last - FIRST_PASSES, :, :]
                 quantise(i, slice(first, last), grouped, a_mx, "a")
 
         def multiply(i):
@@ -259,11 +254,11 @@ def tile_decoder_pb_k_kernel(tc, h7_pre, g7, be7, W8, b8, out):
         for bank in range(GROUP_BANKS):
             transpose_h(1, bank)
         statistics(0)
-        spread(0)
-        copy_w(0)
-        gain_times_mean(0)
         invert_spread(0)
-        scale_and_centre(0)
+        for bank in range(GROUP_BANKS):
+            copy_w(0, bank)
+        scale(0)
+        centre(0)
         shift(0)
 
         for t in range(TOTAL + 3):
@@ -274,18 +269,19 @@ def tile_decoder_pb_k_kernel(tc, h7_pre, g7, be7, W8, b8, out):
             for bank in range(GROUP_BANKS):
                 norm_relu(t, bank)
                 transpose_h(t + 2, bank)
-            spread(t + 1)
-            copy_w(t + 1)
-            regroup_on_scalar(t)
-            add_bias(t - 3)
-            gain_times_mean(t + 1)
-            quantise_w(t, 0)
             invert_spread(t + 1)
+            copy_w(t + 1, 0)
+            copy_w(t + 1, 1)
+            regroup_first(t, nc.scalar.copy, slice(0, SCALAR_ROWS))
+            regroup_first(t - 1, nc.vector.tensor_copy, slice(SCALAR_ROWS, ROWS))
+            add_bias(t - 3)
+            quantise_w(t, 0)
+            scale(t + 1)
             quantise_w(t, 1)
-            scale_and_centre(t + 1)
+            centre(t + 1)
             quantise_a(t - 1, 0, 1)
-            quantise_a(t - 1, 1, 2)
             shift(t + 1)
+            quantise_a(t - 1, 1, 2)
             quantise_a(t - 1, 2, 4)
             multiply(t - 1)
 

@@ -37,6 +37,7 @@ HALF_BLOCKS = BLOCKS // 2
 FIRST_PASSES = 1
 SCALAR_ROWS = 64
 STATS = 6
+LAG = 2
 AHEAD = 4
 
 FLOPS = 2 * BLOCKS * ROWS * CHANNELS * K
@@ -47,31 +48,39 @@ def tile_decoder_pb_k_kernel(tc, h7_pre, g7, be7, W8, b8, out):
     with ExitStack() as ctx:
         ctx.enter_context(tc.manual_schedule())
         const = ctx.enter_context(tc.tile_pool(name="const", bufs=1))
-        loads = ctx.enter_context(tc.tile_pool(name="loads", bufs=AHEAD + 2))
+        h_loads = ctx.enter_context(tc.tile_pool(name="h_loads", bufs=AHEAD + 2))
+        w_loads = ctx.enter_context(tc.tile_pool(name="w_loads", bufs=AHEAD + 3))
         small = ctx.enter_context(tc.tile_pool(name="small", bufs=3))
         work = ctx.enter_context(tc.tile_pool(name="work", bufs=3))
         single = ctx.enter_context(tc.tile_pool(name="single", bufs=1))
         quant = ctx.enter_context(tc.tile_pool(name="quant", bufs=4))
-        psum_h = ctx.enter_context(tc.psum_pool(name="psum_h", bufs=2 * GROUP_BANKS))
-        psum_w = ctx.enter_context(tc.psum_pool(name="psum_w", bufs=GROUP_BANKS))
-        psum_y = ctx.enter_context(tc.psum_pool(name="psum_y", bufs=2))
+        psum_h = ctx.enter_context(tc.psum_pool(name="psum_h", bufs=(LAG + 1) * GROUP_BANKS))
+        psum_w = ctx.enter_context(tc.psum_pool(name="psum_w", bufs=1))
+        psum_y = ctx.enter_context(tc.psum_pool(name="psum_y", bufs=1))
 
         h_in, w_in, h_banks, w_banks, stats_of, scale_of, shift_of = {}, {}, {}, {}, {}, {}, {}
         inverse_of, centre_of = {}, {}
         a_first_of = {}
         planes_of, a_grouped_of, w_grouped_of, a_mx, w_mx, y_of = {}, {}, {}, {}, {}, {}
 
-        def load(i):
-            if i >= TOTAL:
-                return
-            b, k_cols = i // GROUPS, slice((i % GROUPS) * GROUP_K, (i % GROUPS + 1) * GROUP_K)
-            h_in[i] = loads.tile([P, GROUP_K], BF16, name="h_sb")
-            nc.sync.dma_start(out=h_in[i][:], in_=h7_pre[b, :, k_cols])
-            w_in[i] = loads.tile([P, GROUP_K], BF16, name="w_sb")
-            nc.sync.dma_start(out=w_in[i][:], in_=W8[b, :, k_cols])
+        def k_columns(i):
+            return i // GROUPS, slice((i % GROUPS) * GROUP_K, (i % GROUPS + 1) * GROUP_K)
 
-        for i in range(AHEAD):
-            load(i)
+        def load_h(i):
+            if 0 <= i < TOTAL:
+                b, k_cols = k_columns(i)
+                h_in[i] = h_loads.tile([P, GROUP_K], BF16, name="h_sb")
+                nc.sync.dma_start(out=h_in[i][:], in_=h7_pre[b, :, k_cols])
+
+        def load_w(i):
+            if 0 <= i < TOTAL:
+                b, k_cols = k_columns(i)
+                w_in[i] = w_loads.tile([P, GROUP_K], BF16, name="w_sb")
+                nc.sync.dma_start(out=w_in[i][:], in_=W8[b, :, k_cols])
+
+        for i in range(AHEAD + LAG + 1):
+            load_h(i)
+            load_w(i - LAG)
 
         ident = const.tile([P, P], F32)
         make_identity(nc, ident[:])
@@ -102,18 +111,18 @@ def tile_decoder_pb_k_kernel(tc, h7_pre, g7, be7, W8, b8, out):
 
         def transpose_h(i, bank):
             if i < TOTAL:
-                h_banks[i] = h_banks.get(i, []) + [transpose_words(h_in[i], bank, psum_h, "hT")]
+                h_banks[i, bank] = transpose_words(h_in[i], bank, psum_h, "hT")
 
-        def transpose_w(i):
+        def transpose_w(i, bank):
             if i < TOTAL:
-                w_banks[i] = [transpose_words(w_in[i], bank, psum_w, "wT") for bank in range(GROUP_BANKS)]
+                w_banks[i, bank] = transpose_words(w_in[i], bank, psum_w, "wT")
 
         def statistics(i):
             if i >= TOTAL:
                 return
             stats_of[i] = small.tile([P, GROUP_TILES, STATS], F32, name="stats")
             for j in range(GROUP_TILES):
-                nc.vector.bn_stats(out=stats_of[i][:, j, :], in_=h_banks[i][j // BANK_TILES][:, j % BANK_TILES, :].bitcast(BF16))
+                nc.vector.bn_stats(out=stats_of[i][:, j, :], in_=h_banks[i, j // BANK_TILES][:, j % BANK_TILES, :].bitcast(BF16))
 
         def invert_spread(i):
             if i >= TOTAL:
@@ -155,7 +164,7 @@ def tile_decoder_pb_k_kernel(tc, h7_pre, g7, be7, W8, b8, out):
                 planes_of[i] = work.tile([P, GROUP_PASSES, PACK, ROWS], BF16, name="a_planes")
             for j in range(bank * BANK_TILES, (bank + 1) * BANK_TILES):
                 g, u = j // PASS_TILES, j % PASS_TILES
-                pairs = h_banks[i][j // BANK_TILES][:, j % BANK_TILES, :].bitcast(BF16).rearrange("p (n e) -> p n e", e=PAIR)
+                pairs = h_banks[i, bank][:, j % BANK_TILES, :].bitcast(BF16).rearrange("p (n e) -> p n e", e=PAIR)
                 for e in range(PAIR):
                     col = j * PAIR + e
                     nc.scalar.activation(
@@ -197,7 +206,7 @@ def tile_decoder_pb_k_kernel(tc, h7_pre, g7, be7, W8, b8, out):
             grouped_words = w_grouped_of[i][:].bitcast(F32)
             nc.scalar.copy(
                 out=grouped_words[:, bank * BANK_PASSES : (bank + 1) * BANK_PASSES, :, :],
-                in_=w_banks[i][bank][:].rearrange("p (g u) c -> p g c u", u=PASS_TILES),
+                in_=w_banks[i, bank][:].rearrange("p (g u) c -> p g c u", u=PASS_TILES),
             )
 
         def quantise(i, passes, grouped, mx_of, name):
@@ -248,39 +257,42 @@ def tile_decoder_pb_k_kernel(tc, h7_pre, g7, be7, W8, b8, out):
                 b = i // GROUPS
                 nc.vector.tensor_add(out=y_sb[:, b, :], in0=y_of[b][:], in1=bias[:, b * CHANNELS : (b + 1) * CHANNELS])
 
+        for i in range(LAG):
+            for bank in range(GROUP_BANKS):
+                transpose_h(i, bank)
+        transpose_w(0, 0)
         for bank in range(GROUP_BANKS):
-            transpose_h(0, bank)
-        transpose_w(0)
-        for bank in range(GROUP_BANKS):
-            transpose_h(1, bank)
+            transpose_h(LAG, bank)
         statistics(0)
         invert_spread(0)
-        for bank in range(GROUP_BANKS):
-            copy_w(0, bank)
         scale(0)
         centre(0)
         shift(0)
+        statistics(1)
 
-        for t in range(TOTAL + 3):
-            load(t + AHEAD)
-            transpose_w(t + 1)
+        for t in range(TOTAL + 2):
+            load_h(t + LAG + 1 + AHEAD)
+            load_w(t + 1 + AHEAD)
             regroup_on_gpsimd(t - 1)
-            statistics(t + 1)
-            for bank in range(GROUP_BANKS):
-                norm_relu(t, bank)
-                transpose_h(t + 2, bank)
+            statistics(t + 2)
+            norm_relu(t, 0)
             invert_spread(t + 1)
-            copy_w(t + 1, 0)
-            copy_w(t + 1, 1)
+            transpose_h(t + LAG + 1, 0)
+            copy_w(t, 0)
+            transpose_w(t, 1)
+            norm_relu(t, 1)
+            transpose_h(t + LAG + 1, 1)
+            copy_w(t, 1)
+            transpose_w(t + 1, 0)
             regroup_first(t, nc.scalar.copy, slice(0, SCALAR_ROWS))
             regroup_first(t - 1, nc.vector.tensor_copy, slice(SCALAR_ROWS, ROWS))
-            add_bias(t - 3)
-            quantise_w(t, 0)
             scale(t + 1)
-            quantise_w(t, 1)
+            quantise_w(t - 1, 0)
             centre(t + 1)
-            quantise_a(t - 1, 0, 1)
+            quantise_w(t - 1, 1)
             shift(t + 1)
+            add_bias(t - 2)
+            quantise_a(t - 1, 0, 1)
             quantise_a(t - 1, 1, 2)
             quantise_a(t - 1, 2, 4)
             multiply(t - 1)

@@ -34,8 +34,7 @@ GROUPS = K // GROUP_K
 TOTAL = BLOCKS * GROUPS
 BLOCK_TILES = K // TILE_K
 HALF_BLOCKS = BLOCKS // 2
-FIRST_PASSES = 1
-SCALAR_ROWS = 64
+VECTOR_PASSES = 1
 STATS = 6
 LAG = 2
 AHEAD = 4
@@ -60,7 +59,6 @@ def tile_decoder_pb_k_kernel(tc, h7_pre, g7, be7, W8, b8, out):
 
         h_in, w_in, h_banks, w_banks, stats_of, scale_of, shift_of = {}, {}, {}, {}, {}, {}, {}
         inverse_of, centre_of = {}, {}
-        a_first_of = {}
         planes_of, a_grouped_of, w_grouped_of, a_mx, w_mx, y_of = {}, {}, {}, {}, {}, {}
 
         def k_columns(i):
@@ -70,7 +68,13 @@ def tile_decoder_pb_k_kernel(tc, h7_pre, g7, be7, W8, b8, out):
             if 0 <= i < TOTAL:
                 b, k_cols = k_columns(i)
                 h_in[i] = h_loads.tile([P, GROUP_K], BF16, name="h_sb")
-                nc.sync.dma_start(out=h_in[i][:], in_=h7_pre[b, :, k_cols])
+                pieces = GROUP_BANKS if i == 0 else 1
+                width = GROUP_K // pieces
+                for c in range(pieces):
+                    nc.sync.dma_start(
+                        out=h_in[i][:, c * width : (c + 1) * width],
+                        in_=h7_pre[b, :, k_cols.start + c * width : k_cols.start + (c + 1) * width],
+                    )
 
         def load_w(i):
             if 0 <= i < TOTAL:
@@ -91,15 +95,16 @@ def tile_decoder_pb_k_kernel(tc, h7_pre, g7, be7, W8, b8, out):
                 out=affine_rows[:, 2 * v : 2 * v + 2, :],
                 in_=vec.rearrange("b (j c) -> (b j) c", c=TILE_K).rearrange("(s r) c -> r s c", s=2),
             )
-        bias = const.tile([P, BLOCKS * CHANNELS], BF16)
-        nc.scalar.dma_start(out=bias[:], in_=b8.rearrange("b c -> (b c)").partition_broadcast(P))
-        affine_ps = psum_w.tile([P, BANK_TILES, P], F32, name="wT")
-        for s in range(4):
-            nc.tensor.transpose(affine_ps[:, s, :], affine_rows[:, s, :].bitcast(F32), ident[:])
         affine_words = const.tile([P, 4, P], F32)
-        nc.vector.tensor_copy(out=affine_words[:], in_=affine_ps[:])
         affine = affine_words[:].bitcast(BF16)
+        bias = const.tile([P, BLOCKS * CHANNELS], BF16)
         y_sb = const.tile([P, BLOCKS, CHANNELS], F32)
+
+        def transpose_affine():
+            affine_ps = psum_w.tile([P, BANK_TILES, P], F32, name="wT")
+            for s in range(4):
+                nc.tensor.transpose(affine_ps[:, s, :], affine_rows[:, s, :].bitcast(F32), ident[:])
+            nc.vector.tensor_copy(out=affine_words[:], in_=affine_ps[:])
 
         def transpose_words(src, bank, pool, name):
             words = src[:].bitcast(F32)
@@ -178,24 +183,22 @@ def tile_decoder_pb_k_kernel(tc, h7_pre, g7, be7, W8, b8, out):
         def regroup_on_gpsimd(i):
             if not 0 <= i < TOTAL:
                 return
-            a_grouped_of[i] = single.tile([P, GROUP_PASSES - FIRST_PASSES, ROWS, PACK], BF16, name="a_grouped", align_bytes=64)
+            a_grouped_of[i] = single.tile([P, GROUP_PASSES, ROWS, PACK], BF16, name="a_grouped", align_bytes=64)
             nc.gpsimd.tensor_scalar(
-                out=a_grouped_of[i][:],
-                in0=planes_of[i][:, FIRST_PASSES:, :, :].rearrange("p g t n -> p g n t"),
+                out=a_grouped_of[i][:, VECTOR_PASSES:, :, :],
+                in0=planes_of[i][:, VECTOR_PASSES:, :, :].rearrange("p g t n -> p g n t"),
                 scalar1=1.0,
                 scalar2=0.0,
                 op0=ALU.mult,
                 op1=ALU.add,
             )
 
-        def regroup_first(i, copy, rows):
+        def regroup_on_vector(i):
             if not 0 <= i < TOTAL:
                 return
-            if i not in a_first_of:
-                a_first_of[i] = work.tile([P, FIRST_PASSES, ROWS, PACK], BF16, name="a_first", align_bytes=64)
-            copy(
-                out=a_first_of[i][:, :, rows, :].rearrange("p g (c i) t -> p g c t i", i=4),
-                in_=planes_of[i][:, :FIRST_PASSES, :, rows].rearrange("p g t (c i) -> p g c t i", i=4),
+            nc.vector.tensor_copy(
+                out=a_grouped_of[i][:, :VECTOR_PASSES, :, :].rearrange("p g (c i) t -> p g c t i", i=4),
+                in_=planes_of[i][:, :VECTOR_PASSES, :, :].rearrange("p g t (c i) -> p g c t i", i=4),
             )
 
         def copy_w(i, bank):
@@ -209,31 +212,21 @@ def tile_decoder_pb_k_kernel(tc, h7_pre, g7, be7, W8, b8, out):
                 in_=w_banks[i, bank][:].rearrange("p (g u) c -> p g c u", u=PASS_TILES),
             )
 
-        def quantise(i, passes, grouped, mx_of, name):
-            if i not in mx_of:
+        def quantise(i, bank, grouped_of, mx_of, name):
+            if not 0 <= i < TOTAL:
+                return
+            if bank == 0:
                 mx_of[i] = (
                     quant.tile([P, GROUP_PASSES, P], U32, name=name + "_codes", align_bytes=64),
                     quant.tile([P, GROUP_PASSES, P], U8, name=name + "_scales", align_bytes=64),
                 )
             codes, scales = mx_of[i]
+            passes = slice(bank * BANK_PASSES, (bank + 1) * BANK_PASSES)
             nc.vector.quantize_mx(
                 out=codes[:, passes, :].rearrange("p g n -> p (g n)").bitcast(FP8X4),
                 scales=scales[:, passes, :].rearrange("p g n -> p (g n)"),
-                in_=grouped.rearrange("p g n t -> p (g n t)"),
+                in_=grouped_of[i][:, passes, :, :].rearrange("p g n t -> p (g n t)"),
             )
-
-        def quantise_w(i, bank):
-            if 0 <= i < TOTAL:
-                passes = slice(bank * BANK_PASSES, (bank + 1) * BANK_PASSES)
-                quantise(i, passes, w_grouped_of[i][:, passes, :, :], w_mx, "w")
-
-        def quantise_a(i, first, last):
-            if 0 <= i < TOTAL:
-                if first < FIRST_PASSES:
-                    grouped = a_first_of[i][:, first:last, :, :]
-                else:
-                    grouped = a_grouped_of[i][:, first - FIRST_PASSES : last - FIRST_PASSES, :, :]
-                quantise(i, slice(first, last), grouped, a_mx, "a")
 
         def multiply(i):
             if not 0 <= i < TOTAL:
@@ -257,14 +250,15 @@ def tile_decoder_pb_k_kernel(tc, h7_pre, g7, be7, W8, b8, out):
                 b = i // GROUPS
                 nc.vector.tensor_add(out=y_sb[:, b, :], in0=y_of[b][:], in1=bias[:, b * CHANNELS : (b + 1) * CHANNELS])
 
-        for i in range(LAG):
+        for bank in range(GROUP_BANKS):
+            transpose_h(0, bank)
+        statistics(0)
+        invert_spread(0)
+        transpose_affine()
+        for i in range(1, LAG + 1):
             for bank in range(GROUP_BANKS):
                 transpose_h(i, bank)
         transpose_w(0, 0)
-        for bank in range(GROUP_BANKS):
-            transpose_h(LAG, bank)
-        statistics(0)
-        invert_spread(0)
         scale(0)
         centre(0)
         shift(0)
@@ -273,6 +267,8 @@ def tile_decoder_pb_k_kernel(tc, h7_pre, g7, be7, W8, b8, out):
         for t in range(TOTAL + 2):
             load_h(t + LAG + 1 + AHEAD)
             load_w(t + 1 + AHEAD)
+            if t == 0:
+                nc.sync.dma_start(out=bias[:], in_=b8.rearrange("b c -> (b c)").partition_broadcast(P))
             regroup_on_gpsimd(t - 1)
             statistics(t + 2)
             norm_relu(t, 0)
@@ -284,17 +280,15 @@ def tile_decoder_pb_k_kernel(tc, h7_pre, g7, be7, W8, b8, out):
             transpose_h(t + LAG + 1, 1)
             copy_w(t, 1)
             transpose_w(t + 1, 0)
-            regroup_first(t, nc.scalar.copy, slice(0, SCALAR_ROWS))
-            regroup_first(t - 1, nc.vector.tensor_copy, slice(SCALAR_ROWS, ROWS))
+            regroup_on_vector(t - 1)
             scale(t + 1)
-            quantise_w(t - 1, 0)
+            quantise(t - 1, 0, w_grouped_of, w_mx, "w")
             centre(t + 1)
-            quantise_w(t - 1, 1)
+            quantise(t - 1, 1, w_grouped_of, w_mx, "w")
             shift(t + 1)
             add_bias(t - 2)
-            quantise_a(t - 1, 0, 1)
-            quantise_a(t - 1, 1, 2)
-            quantise_a(t - 1, 2, 4)
+            quantise(t - 1, 0, a_grouped_of, a_mx, "a")
+            quantise(t - 1, 1, a_grouped_of, a_mx, "a")
             multiply(t - 1)
 
         last = BLOCKS - 1

@@ -32,6 +32,7 @@ GROUP_BANKS = GROUP_TILES // BANK_TILES
 GROUP_COLS = GROUP_TILES * PAIR
 GROUPS = K // GROUP_K
 TOTAL = BLOCKS * GROUPS
+LAST = TOTAL - 1
 BLOCK_TILES = K // TILE_K
 HALF_BLOCKS = BLOCKS // 2
 VECTOR_PASSES = 1
@@ -162,14 +163,12 @@ def tile_decoder_pb_k_kernel(tc, h7_pre, g7, be7, W8, b8, out):
                 shift_of[i] = small.tile([P, GROUP_COLS], F32, name="shift_k")
                 nc.vector.tensor_sub(out=shift_of[i][:], in0=beta, in1=centre_of[i][:])
 
-        def norm_relu(i, bank):
-            if i >= TOTAL:
-                return
-            if bank == 0:
+        def norm_relu(i, g):
+            if g == 0:
                 planes_of[i] = work.tile([P, GROUP_PASSES, PACK, ROWS], BF16, name="a_planes")
-            for j in range(bank * BANK_TILES, (bank + 1) * BANK_TILES):
-                g, u = j // PASS_TILES, j % PASS_TILES
-                pairs = h_banks[i, bank][:, j % BANK_TILES, :].bitcast(BF16).rearrange("p (n e) -> p n e", e=PAIR)
+            for u in range(PASS_TILES):
+                j = g * PASS_TILES + u
+                pairs = h_banks[i, j // BANK_TILES][:, j % BANK_TILES, :].bitcast(BF16).rearrange("p (n e) -> p n e", e=PAIR)
                 for e in range(PAIR):
                     col = j * PAIR + e
                     nc.scalar.activation(
@@ -181,7 +180,7 @@ def tile_decoder_pb_k_kernel(tc, h7_pre, g7, be7, W8, b8, out):
                     )
 
         def regroup_on_gpsimd(i):
-            if not 0 <= i < TOTAL:
+            if not 0 <= i < LAST:
                 return
             a_grouped_of[i] = single.tile([P, GROUP_PASSES, ROWS, PACK], BF16, name="a_grouped", align_bytes=64)
             nc.gpsimd.tensor_scalar(
@@ -193,12 +192,10 @@ def tile_decoder_pb_k_kernel(tc, h7_pre, g7, be7, W8, b8, out):
                 op1=ALU.add,
             )
 
-        def regroup_on_vector(i):
-            if not 0 <= i < TOTAL:
-                return
+        def regroup_on_vector(i, passes):
             nc.vector.tensor_copy(
-                out=a_grouped_of[i][:, :VECTOR_PASSES, :, :].rearrange("p g (c i) t -> p g c t i", i=4),
-                in_=planes_of[i][:, :VECTOR_PASSES, :, :].rearrange("p g t (c i) -> p g c t i", i=4),
+                out=a_grouped_of[i][:, passes, :, :].rearrange("p g (c i) t -> p g c t i", i=4),
+                in_=planes_of[i][:, passes, :, :].rearrange("p g t (c i) -> p g c t i", i=4),
             )
 
         def copy_w(i, bank):
@@ -212,21 +209,24 @@ def tile_decoder_pb_k_kernel(tc, h7_pre, g7, be7, W8, b8, out):
                 in_=w_banks[i, bank][:].rearrange("p (g u) c -> p g c u", u=PASS_TILES),
             )
 
-        def quantise(i, bank, grouped_of, mx_of, name):
-            if not 0 <= i < TOTAL:
-                return
-            if bank == 0:
+        def quantise(i, first, last, grouped_of, mx_of, name):
+            if i not in mx_of:
                 mx_of[i] = (
                     quant.tile([P, GROUP_PASSES, P], U32, name=name + "_codes", align_bytes=64),
                     quant.tile([P, GROUP_PASSES, P], U8, name=name + "_scales", align_bytes=64),
                 )
             codes, scales = mx_of[i]
-            passes = slice(bank * BANK_PASSES, (bank + 1) * BANK_PASSES)
             nc.vector.quantize_mx(
-                out=codes[:, passes, :].rearrange("p g n -> p (g n)").bitcast(FP8X4),
-                scales=scales[:, passes, :].rearrange("p g n -> p (g n)"),
-                in_=grouped_of[i][:, passes, :, :].rearrange("p g n t -> p (g n t)"),
+                out=codes[:, first:last, :].rearrange("p g n -> p (g n)").bitcast(FP8X4),
+                scales=scales[:, first:last, :].rearrange("p g n -> p (g n)"),
+                in_=grouped_of[i][:, first:last, :, :].rearrange("p g n t -> p (g n t)"),
             )
+
+        def quantise_a(i, first, last):
+            quantise(i, first, last, a_grouped_of, a_mx, "a")
+
+        def quantise_w(i, bank):
+            quantise(i, bank * BANK_PASSES, (bank + 1) * BANK_PASSES, w_grouped_of, w_mx, "w")
 
         def multiply(i):
             if not 0 <= i < TOTAL:
@@ -264,32 +264,56 @@ def tile_decoder_pb_k_kernel(tc, h7_pre, g7, be7, W8, b8, out):
         shift(0)
         statistics(1)
 
-        for t in range(TOTAL + 2):
+        for t in range(TOTAL):
             load_h(t + LAG + 1 + AHEAD)
             load_w(t + 1 + AHEAD)
             if t == 0:
                 nc.sync.dma_start(out=bias[:], in_=b8.rearrange("b c -> (b c)").partition_broadcast(P))
             regroup_on_gpsimd(t - 1)
             statistics(t + 2)
-            norm_relu(t, 0)
-            invert_spread(t + 1)
-            transpose_h(t + LAG + 1, 0)
-            copy_w(t, 0)
-            transpose_w(t, 1)
-            norm_relu(t, 1)
-            transpose_h(t + LAG + 1, 1)
-            copy_w(t, 1)
-            transpose_w(t + 1, 0)
-            regroup_on_vector(t - 1)
-            scale(t + 1)
-            quantise(t - 1, 0, w_grouped_of, w_mx, "w")
-            centre(t + 1)
-            quantise(t - 1, 1, w_grouped_of, w_mx, "w")
-            shift(t + 1)
-            add_bias(t - 2)
-            quantise(t - 1, 0, a_grouped_of, a_mx, "a")
-            quantise(t - 1, 1, a_grouped_of, a_mx, "a")
-            multiply(t - 1)
+            if t < TOTAL:
+                norm_relu(t, 0)
+                norm_relu(t, 1)
+                transpose_h(t + LAG + 1, 0)
+                invert_spread(t + 1)
+                copy_w(t, 0)
+                transpose_w(t, 1)
+                norm_relu(t, 2)
+                if t < LAST:
+                    norm_relu(t, 3)
+                    transpose_h(t + LAG + 1, 1)
+                    copy_w(t, 1)
+                    transpose_w(t + 1, 0)
+                else:
+                    copy_w(t, 1)
+                    norm_relu(t, 3)
+            if 0 <= t - 1 < LAST:
+                regroup_on_vector(t - 1, slice(0, VECTOR_PASSES))
+                scale(t + 1)
+                quantise_w(t - 1, 0)
+                centre(t + 1)
+                add_bias(t - 2)
+                quantise_a(t - 1, 0, GROUP_PASSES)
+                shift(t + 1)
+                quantise_w(t - 1, 1)
+                multiply(t - 1)
+            elif t < LAST:
+                scale(t + 1)
+                centre(t + 1)
+                shift(t + 1)
+
+        a_grouped_of[LAST] = single.tile([P, GROUP_PASSES, ROWS, PACK], BF16, name="a_grouped", align_bytes=64)
+        regroup_on_vector(LAST, slice(0, 1))
+        regroup_on_vector(LAST, slice(1, 2))
+        quantise_w(LAST, 0)
+        quantise_a(LAST, 0, 2)
+        regroup_on_vector(LAST, slice(2, 3))
+        quantise_w(LAST, 1)
+        regroup_on_vector(LAST, slice(3, 4))
+        quantise_a(LAST, 2, 3)
+        quantise_a(LAST, 3, 4)
+        multiply(LAST)
+        add_bias(LAST)
 
         last = BLOCKS - 1
         nc.scalar.activation(out=y_sb[:, :last, :], in_=y_sb[:, :last, :], func=ACT.Sigmoid)

@@ -37,6 +37,7 @@ BLOCK_TILES = K // TILE_K
 HALF_BLOCKS = BLOCKS // 2
 VECTOR_PASSES = 1
 STATS = 6
+SCALAR_ROWS = 64
 LAG = 2
 AHEAD = 4
 
@@ -182,7 +183,6 @@ def tile_decoder_pb_k_kernel(tc, h7_pre, g7, be7, W8, b8, out):
         def regroup_on_gpsimd(i):
             if not 0 <= i < LAST:
                 return
-            a_grouped_of[i] = single.tile([P, GROUP_PASSES, ROWS, PACK], BF16, name="a_grouped", align_bytes=64)
             nc.gpsimd.tensor_scalar(
                 out=a_grouped_of[i][:, VECTOR_PASSES:, :, :],
                 in0=planes_of[i][:, VECTOR_PASSES:, :, :].rearrange("p g t n -> p g n t"),
@@ -192,10 +192,10 @@ def tile_decoder_pb_k_kernel(tc, h7_pre, g7, be7, W8, b8, out):
                 op1=ALU.add,
             )
 
-        def regroup_on_vector(i, passes):
-            nc.vector.tensor_copy(
-                out=a_grouped_of[i][:, passes, :, :].rearrange("p g (c i) t -> p g c t i", i=4),
-                in_=planes_of[i][:, passes, :, :].rearrange("p g t (c i) -> p g c t i", i=4),
+        def regroup(i, copy, passes, rows):
+            copy(
+                out=a_grouped_of[i][:, passes, rows, :].rearrange("p g (c i) t -> p g c t i", i=4),
+                in_=planes_of[i][:, passes, :, rows].rearrange("p g t (c i) -> p g c t i", i=4),
             )
 
         def copy_w(i, bank):
@@ -288,7 +288,7 @@ def tile_decoder_pb_k_kernel(tc, h7_pre, g7, be7, W8, b8, out):
                     copy_w(t, 1)
                     norm_relu(t, 3)
             if 0 <= t - 1 < LAST:
-                regroup_on_vector(t - 1, slice(0, VECTOR_PASSES))
+                regroup(t - 1, nc.vector.tensor_copy, slice(0, VECTOR_PASSES), slice(SCALAR_ROWS, ROWS))
                 scale(t + 1)
                 quantise_w(t - 1, 0)
                 centre(t + 1)
@@ -302,14 +302,18 @@ def tile_decoder_pb_k_kernel(tc, h7_pre, g7, be7, W8, b8, out):
                 centre(t + 1)
                 shift(t + 1)
 
+            if t < LAST:
+                a_grouped_of[t] = single.tile([P, GROUP_PASSES, ROWS, PACK], BF16, name="a_grouped", align_bytes=64)
+                regroup(t, nc.scalar.copy, slice(0, VECTOR_PASSES), slice(0, SCALAR_ROWS))
+
         a_grouped_of[LAST] = single.tile([P, GROUP_PASSES, ROWS, PACK], BF16, name="a_grouped", align_bytes=64)
-        regroup_on_vector(LAST, slice(0, 1))
-        regroup_on_vector(LAST, slice(1, 2))
+        regroup(LAST, nc.vector.tensor_copy, slice(0, 1), slice(0, ROWS))
+        regroup(LAST, nc.vector.tensor_copy, slice(1, 2), slice(0, ROWS))
         quantise_w(LAST, 0)
         quantise_a(LAST, 0, 2)
-        regroup_on_vector(LAST, slice(2, 3))
+        regroup(LAST, nc.vector.tensor_copy, slice(2, 3), slice(0, ROWS))
         quantise_w(LAST, 1)
-        regroup_on_vector(LAST, slice(3, 4))
+        regroup(LAST, nc.vector.tensor_copy, slice(3, 4), slice(0, ROWS))
         quantise_a(LAST, 2, 3)
         quantise_a(LAST, 3, 4)
         multiply(LAST)

@@ -37,8 +37,9 @@ BLOCK_TILES = K // TILE_K
 HALF_BLOCKS = BLOCKS // 2
 VECTOR_PASSES = 1
 STATS = 6
-SCALAR_ROWS = 64
+SCALAR_ROWS = 32
 LAG = 2
+SHARED = TOTAL - LAG - 1
 AHEAD = 4
 
 FLOPS = 2 * BLOCKS * ROWS * CHANNELS * K
@@ -180,8 +181,30 @@ def tile_decoder_pb_k_kernel(tc, h7_pre, g7, be7, W8, b8, out):
                         scale=scale_of[i][:, col : col + 1],
                     )
 
+        def norm_on_vector(i, g):
+            for u in range(PASS_TILES):
+                j = g * PASS_TILES + u
+                pairs = h_banks[i, j // BANK_TILES][:, j % BANK_TILES, :].bitcast(BF16).rearrange("p (n e) -> p n e", e=PAIR)
+                for e in range(PAIR):
+                    col = j * PAIR + e
+                    nc.vector.tensor_scalar(
+                        out=planes_of[i][:, g, u * PAIR + e, :],
+                        in0=pairs[:, :, e],
+                        scalar1=scale_of[i][:, col : col + 1],
+                        scalar2=shift_of[i][:, col : col + 1],
+                        op0=ALU.mult,
+                        op1=ALU.add,
+                    )
+
+        def regroup_relu(i, g):
+            nc.vector.tensor_scalar_max(
+                out=a_grouped_of[i][:, g : g + 1, :, :].rearrange("p g (c i) t -> p g c t i", i=4),
+                in0=planes_of[i][:, g : g + 1, :, :].rearrange("p g t (c i) -> p g c t i", i=4),
+                scalar1=0.0,
+            )
+
         def regroup_on_gpsimd(i):
-            if not 0 <= i < LAST:
+            if not 0 <= i < SHARED:
                 return
             nc.gpsimd.tensor_scalar(
                 out=a_grouped_of[i][:, VECTOR_PASSES:, :, :],
@@ -273,22 +296,29 @@ def tile_decoder_pb_k_kernel(tc, h7_pre, g7, be7, W8, b8, out):
             statistics(t + 2)
             if t < TOTAL:
                 norm_relu(t, 0)
-                norm_relu(t, 1)
-                transpose_h(t + LAG + 1, 0)
-                invert_spread(t + 1)
-                copy_w(t, 0)
-                transpose_w(t, 1)
-                norm_relu(t, 2)
                 if t < LAST:
+                    norm_relu(t, 1)
+                    transpose_h(t + LAG + 1, 0)
+                    invert_spread(t + 1)
+                    copy_w(t, 0)
+                    transpose_w(t, 1)
+                    norm_relu(t, 2)
                     norm_relu(t, 3)
                     transpose_h(t + LAG + 1, 1)
                     copy_w(t, 1)
                     transpose_w(t + 1, 0)
                 else:
+                    copy_w(t, 0)
+                    transpose_w(t, 1)
+                    norm_relu(t, 1)
                     copy_w(t, 1)
-                    norm_relu(t, 3)
+                    norm_on_vector(t, 2)
+                    norm_on_vector(t, 3)
             if 0 <= t - 1 < LAST:
-                regroup(t - 1, nc.vector.tensor_copy, slice(0, VECTOR_PASSES), slice(SCALAR_ROWS, ROWS))
+                if t - 1 < SHARED:
+                    regroup(t - 1, nc.vector.tensor_copy, slice(0, VECTOR_PASSES), slice(SCALAR_ROWS, ROWS))
+                else:
+                    regroup(t - 1, nc.vector.tensor_copy, slice(0, GROUP_PASSES), slice(0, ROWS))
                 scale(t + 1)
                 quantise_w(t - 1, 0)
                 centre(t + 1)
@@ -302,20 +332,18 @@ def tile_decoder_pb_k_kernel(tc, h7_pre, g7, be7, W8, b8, out):
                 centre(t + 1)
                 shift(t + 1)
 
-            if t < LAST:
-                a_grouped_of[t] = single.tile([P, GROUP_PASSES, ROWS, PACK], BF16, name="a_grouped", align_bytes=64)
+            a_grouped_of[t] = single.tile([P, GROUP_PASSES, ROWS, PACK], BF16, name="a_grouped", align_bytes=64)
+            if t < SHARED:
                 regroup(t, nc.scalar.copy, slice(0, VECTOR_PASSES), slice(0, SCALAR_ROWS))
 
-        a_grouped_of[LAST] = single.tile([P, GROUP_PASSES, ROWS, PACK], BF16, name="a_grouped", align_bytes=64)
+        regroup(LAST, nc.scalar.copy, slice(1, 2), slice(0, ROWS))
+        regroup_relu(LAST, 2)
+        regroup_relu(LAST, 3)
         regroup(LAST, nc.vector.tensor_copy, slice(0, 1), slice(0, ROWS))
-        regroup(LAST, nc.vector.tensor_copy, slice(1, 2), slice(0, ROWS))
+        quantise_a(LAST, 2, 4)
         quantise_w(LAST, 0)
         quantise_a(LAST, 0, 2)
-        regroup(LAST, nc.vector.tensor_copy, slice(2, 3), slice(0, ROWS))
         quantise_w(LAST, 1)
-        regroup(LAST, nc.vector.tensor_copy, slice(3, 4), slice(0, ROWS))
-        quantise_a(LAST, 2, 3)
-        quantise_a(LAST, 3, 4)
         multiply(LAST)
         add_bias(LAST)
 

from contextlib import ExitStack

import concourse.mybir as mybir
from concourse.masks import make_identity

F32 = mybir.dt.float32
BF16 = mybir.dt.bfloat16
U32 = mybir.dt.uint32
U8 = mybir.dt.uint8
FP8X4 = mybir.dt.float8_e4m3fn_x4
ACT = mybir.ActivationFunctionType
ALU = mybir.AluOpType

P = 128
BLOCKS = 8
ROWS = 128
CHANNELS = 128
K = 8192
EPS = 1e-5

PAIR = 2
PACK = 4
TILE_K = PAIR * P
PASS_K = PACK * P
PASS_TILES = PASS_K // TILE_K
BANK_TILES = 4
BANK_PASSES = BANK_TILES // PASS_TILES
GROUP_K = 2048
GROUP_TILES = GROUP_K // TILE_K
GROUP_PASSES = GROUP_K // PASS_K
GROUP_BANKS = GROUP_TILES // BANK_TILES
GROUP_COLS = GROUP_TILES * PAIR
GROUPS = K // GROUP_K
TOTAL = BLOCKS * GROUPS
LAST = TOTAL - 1
BLOCK_TILES = K // TILE_K
HALF_BLOCKS = BLOCKS // 2
VECTOR_PASSES = 1
STATS = 6
SCALAR_ROWS = 32
LAG = 2
SHARED = TOTAL - LAG - 1
AHEAD = 4

FLOPS = 2 * BLOCKS * ROWS * CHANNELS * K


def tile_decoder_pb_k_kernel(tc, h7_pre, g7, be7, W8, b8, out):
    nc = tc.nc
    with ExitStack() as ctx:
        ctx.enter_context(tc.manual_schedule())
        const = ctx.enter_context(tc.tile_pool(name="const", bufs=1))
        h_loads = ctx.enter_context(tc.tile_pool(name="h_loads", bufs=AHEAD + 2))
        w_loads = ctx.enter_context(tc.tile_pool(name="w_loads", bufs=AHEAD + 3))
        small = ctx.enter_context(tc.tile_pool(name="small", bufs=3))
        work = ctx.enter_context(tc.tile_pool(name="work", bufs=3))
        single = ctx.enter_context(tc.tile_pool(name="single", bufs=1))
        quant = ctx.enter_context(tc.tile_pool(name="quant", bufs=4))
        psum_h = ctx.enter_context(tc.psum_pool(name="psum_h", bufs=(LAG + 1) * GROUP_BANKS))
        psum_w = ctx.enter_context(tc.psum_pool(name="psum_w", bufs=1))
        psum_y = ctx.enter_context(tc.psum_pool(name="psum_y", bufs=1))

        h_in, w_in, h_banks, w_banks, stats_of, scale_of, shift_of = {}, {}, {}, {}, {}, {}, {}
        inverse_of, centre_of = {}, {}
        planes_of, a_grouped_of, w_grouped_of, a_mx, w_mx, y_of = {}, {}, {}, {}, {}, {}

        def k_columns(i):
            return i // GROUPS, slice((i % GROUPS) * GROUP_K, (i % GROUPS + 1) * GROUP_K)

        def load_h(i):
            if 0 <= i < TOTAL:
                b, k_cols = k_columns(i)
                h_in[i] = h_loads.tile([P, GROUP_K], BF16, name="h_sb")
                pieces = GROUP_BANKS if i == 0 else 1
                width = GROUP_K // pieces
                for c in range(pieces):
                    nc.sync.dma_start(
                        out=h_in[i][:, c * width : (c + 1) * width],
                        in_=h7_pre[b, :, k_cols.start + c * width : k_cols.start + (c + 1) * width],
                    )

        def load_w(i):
            if 0 <= i < TOTAL:
                b, k_cols = k_columns(i)
                w_in[i] = w_loads.tile([P, GROUP_K], BF16, name="w_sb")
                nc.sync.dma_start(out=w_in[i][:], in_=W8[b, :, k_cols])

        for i in range(AHEAD + LAG + 1):
            load_h(i)
            load_w(i - LAG)

        ident = const.tile([P, P], F32)
        make_identity(nc, ident[:])

        affine_rows = const.tile([P, 4, TILE_K], BF16)
        for v, vec in enumerate((g7, be7)):
            nc.scalar.dma_start(
                out=affine_rows[:, 2 * v : 2 * v + 2, :],
                in_=vec.rearrange("b (j c) -> (b j) c", c=TILE_K).rearrange("(s r) c -> r s c", s=2),
            )
        affine_words = const.tile([P, 4, P], F32)
        affine = affine_words[:].bitcast(BF16)
        bias = const.tile([P, BLOCKS * CHANNELS], BF16)
        y_sb = const.tile([P, BLOCKS, CHANNELS], F32)

        def transpose_affine():
            affine_ps = psum_w.tile([P, BANK_TILES, P], F32, name="wT")
            for s in range(4):
                nc.tensor.transpose(affine_ps[:, s, :], affine_rows[:, s, :].bitcast(F32), ident[:])
            nc.vector.tensor_copy(out=affine_words[:], in_=affine_ps[:])

        def transpose_words(src, bank, pool, name):
            words = src[:].bitcast(F32)
            turned = pool.tile([P, BANK_TILES, P], F32, name=name)
            for s in range(BANK_TILES):
                j = bank * BANK_TILES + s
                nc.tensor.transpose(turned[:, s, :], words[:, j * P : (j + 1) * P], ident[:])
            return turned

        def transpose_h(i, bank):
            if i < TOTAL:
                h_banks[i, bank] = transpose_words(h_in[i], bank, psum_h, "hT")

        def transpose_w(i, bank):
            if i < TOTAL:
                w_banks[i, bank] = transpose_words(w_in[i], bank, psum_w, "wT")

        def statistics(i):
            if i >= TOTAL:
                return
            stats_of[i] = small.tile([P, GROUP_TILES, STATS], F32, name="stats")
            for j in range(GROUP_TILES):
                nc.vector.bn_stats(out=stats_of[i][:, j, :], in_=h_banks[i, j // BANK_TILES][:, j % BANK_TILES, :].bitcast(BF16))

        def invert_spread(i):
            if i >= TOTAL:
                return
            sum_of_squares = stats_of[i][:].rearrange("p j (e f) -> p (j e) f", f=3)[:, :, 2]
            inverse_of[i] = small.tile([P, GROUP_COLS], F32, name="inverse_k")
            nc.scalar.activation(out=inverse_of[i][:], in_=sum_of_squares, func=ACT.Abs_reciprocal_sqrt, bias=EPS, scale=1.0 / ROWS)

        def per_k(i):
            b, grp = i // GROUPS, i % GROUPS
            mean = stats_of[i][:].rearrange("p j (e f) -> p (j e) f", f=3)[:, :, 1]
            first = ((b % HALF_BLOCKS) * BLOCK_TILES + grp * GROUP_TILES) * PAIR
            gain = affine[:, b // HALF_BLOCKS, first : first + GROUP_COLS]
            beta = affine[:, 2 + b // HALF_BLOCKS, first : first + GROUP_COLS]
            return mean, gain, beta

        def scale(i):
            if i < TOTAL:
                mean, gain, beta = per_k(i)
                scale_of[i] = small.tile([P, GROUP_COLS], F32, name="scale_k")
                nc.vector.tensor_mul(out=scale_of[i][:], in0=inverse_of[i][:], in1=gain)

        def centre(i):
            if i < TOTAL:
                mean, gain, beta = per_k(i)
                centre_of[i] = small.tile([P, GROUP_COLS], F32, name="centre_k")
                nc.vector.tensor_mul(out=centre_of[i][:], in0=mean, in1=scale_of[i][:])

        def shift(i):
            if i < TOTAL:
                mean, gain, beta = per_k(i)
                shift_of[i] = small.tile([P, GROUP_COLS], F32, name="shift_k")
                nc.vector.tensor_sub(out=shift_of[i][:], in0=beta, in1=centre_of[i][:])

        def norm_relu(i, g):
            if g == 0:
                planes_of[i] = work.tile([P, GROUP_PASSES, PACK, ROWS], BF16, name="a_planes")
            for u in range(PASS_TILES):
                j = g * PASS_TILES + u
                pairs = h_banks[i, j // BANK_TILES][:, j % BANK_TILES, :].bitcast(BF16).rearrange("p (n e) -> p n e", e=PAIR)
                for e in range(PAIR):
                    col = j * PAIR + e
                    nc.scalar.activation(
                        out=planes_of[i][:, g, u * PAIR + e, :],
                        in_=pairs[:, :, e],
                        func=ACT.Relu,
                        bias=shift_of[i][:, col : col + 1],
                        scale=scale_of[i][:, col : col + 1],
                    )

        def norm_on_vector(i, g):
            for u in range(PASS_TILES):
                j = g * PASS_TILES + u
                pairs = h_banks[i, j // BANK_TILES][:, j % BANK_TILES, :].bitcast(BF16).rearrange("p (n e) -> p n e", e=PAIR)
                for e in range(PAIR):
                    col = j * PAIR + e
                    nc.vector.tensor_scalar(
                        out=planes_of[i][:, g, u * PAIR + e, :],
                        in0=pairs[:, :, e],
                        scalar1=scale_of[i][:, col : col + 1],
                        scalar2=shift_of[i][:, col : col + 1],
                        op0=ALU.mult,
                        op1=ALU.add,
                    )

        def regroup_relu(i, g):
            nc.vector.tensor_scalar_max(
                out=a_grouped_of[i][:, g : g + 1, :, :].rearrange("p g (c i) t -> p g c t i", i=4),
                in0=planes_of[i][:, g : g + 1, :, :].rearrange("p g t (c i) -> p g c t i", i=4),
                scalar1=0.0,
            )

        def regroup_on_gpsimd(i):
            if not 0 <= i < SHARED:
                return
            nc.gpsimd.tensor_scalar(
                out=a_grouped_of[i][:, VECTOR_PASSES:, :, :],
                in0=planes_of[i][:, VECTOR_PASSES:, :, :].rearrange("p g t n -> p g n t"),
                scalar1=1.0,
                scalar2=0.0,
                op0=ALU.mult,
                op1=ALU.add,
            )

        def regroup(i, copy, passes, rows):
            copy(
                out=a_grouped_of[i][:, passes, rows, :].rearrange("p g (c i) t -> p g c t i", i=4),
                in_=planes_of[i][:, passes, :, rows].rearrange("p g t (c i) -> p g c t i", i=4),
            )

        def copy_w(i, bank):
            if i >= TOTAL:
                return
            if bank == 0:
                w_grouped_of[i] = work.tile([P, GROUP_PASSES, CHANNELS, PACK], BF16, name="w_grouped", align_bytes=64)
            grouped_words = w_grouped_of[i][:].bitcast(F32)
            nc.scalar.copy(
                out=grouped_words[:, bank * BANK_PASSES : (bank + 1) * BANK_PASSES, :, :],
                in_=w_banks[i, bank][:].rearrange("p (g u) c -> p g c u", u=PASS_TILES),
            )

        def quantise(i, first, last, grouped_of, mx_of, name):
            if i not in mx_of:
                mx_of[i] = (
                    quant.tile([P, GROUP_PASSES, P], U32, name=name + "_codes", align_bytes=64),
                    quant.tile([P, GROUP_PASSES, P], U8, name=name + "_scales", align_bytes=64),
                )
            codes, scales = mx_of[i]
            nc.vector.quantize_mx(
                out=codes[:, first:last, :].rearrange("p g n -> p (g n)").bitcast(FP8X4),
                scales=scales[:, first:last, :].rearrange("p g n -> p (g n)"),
                in_=grouped_of[i][:, first:last, :, :].rearrange("p g n t -> p (g n t)"),
            )

        def quantise_a(i, first, last):
            quantise(i, first, last, a_grouped_of, a_mx, "a")

        def quantise_w(i, bank):
            quantise(i, bank * BANK_PASSES, (bank + 1) * BANK_PASSES, w_grouped_of, w_mx, "w")

        def multiply(i):
            if not 0 <= i < TOTAL:
                return
            b, grp = i // GROUPS, i % GROUPS
            if grp == 0:
                y_of[b] = psum_y.tile([P, CHANNELS], F32, name="y_ps")
            for g in range(GROUP_PASSES):
                nc.tensor.matmul_mx(
                    out=y_of[b][:],
                    lhsT=a_mx[i][0][:, g, :].bitcast(FP8X4),
                    lhsT_scale=a_mx[i][1][:, g, :],
                    rhs=w_mx[i][0][:, g, :].bitcast(FP8X4),
                    rhs_scale=w_mx[i][1][:, g, :],
                    start=(grp == 0 and g == 0),
                    stop=(grp == GROUPS - 1 and g == GROUP_PASSES - 1),
                )

        def add_bias(i):
            if 0 <= i < TOTAL and i % GROUPS == GROUPS - 1:
                b = i // GROUPS
                nc.vector.tensor_add(out=y_sb[:, b, :], in0=y_of[b][:], in1=bias[:, b * CHANNELS : (b + 1) * CHANNELS])

        for bank in range(GROUP_BANKS):
            transpose_h(0, bank)
        statistics(0)
        invert_spread(0)
        transpose_affine()
        for i in range(1, LAG + 1):
            for bank in range(GROUP_BANKS):
                transpose_h(i, bank)
        transpose_w(0, 0)
        scale(0)
        centre(0)
        shift(0)
        statistics(1)

        for t in range(TOTAL):
            load_h(t + LAG + 1 + AHEAD)
            load_w(t + 1 + AHEAD)
            if t == 0:
                nc.sync.dma_start(out=bias[:], in_=b8.rearrange("b c -> (b c)").partition_broadcast(P))
            regroup_on_gpsimd(t - 1)
            statistics(t + 2)
            if t < TOTAL:
                norm_relu(t, 0)
                if t < LAST:
                    norm_relu(t, 1)
                    transpose_h(t + LAG + 1, 0)
                    invert_spread(t + 1)
                    copy_w(t, 0)
                    transpose_w(t, 1)
                    norm_relu(t, 2)
                    norm_relu(t, 3)
                    transpose_h(t + LAG + 1, 1)
                    copy_w(t, 1)
                    transpose_w(t + 1, 0)
                else:
                    copy_w(t, 0)
                    transpose_w(t, 1)
                    norm_relu(t, 1)
                    copy_w(t, 1)
                    norm_on_vector(t, 2)
                    norm_on_vector(t, 3)
            if 0 <= t - 1 < LAST:
                if t - 1 < SHARED:
                    regroup(t - 1, nc.vector.tensor_copy, slice(0, VECTOR_PASSES), slice(SCALAR_ROWS, ROWS))
                else:
                    regroup(t - 1, nc.vector.tensor_copy, slice(0, GROUP_PASSES), slice(0, ROWS))
                scale(t + 1)
                quantise_w(t - 1, 0)
                centre(t + 1)
                add_bias(t - 2)
                quantise_a(t - 1, 0, GROUP_PASSES)
                shift(t + 1)
                quantise_w(t - 1, 1)
                multiply(t - 1)
            elif t < LAST:
                scale(t + 1)
                centre(t + 1)
                shift(t + 1)

            a_grouped_of[t] = single.tile([P, GROUP_PASSES, ROWS, PACK], BF16, name="a_grouped", align_bytes=64)
            if t < SHARED:
                regroup(t, nc.scalar.copy, slice(0, VECTOR_PASSES), slice(0, SCALAR_ROWS))

        regroup(LAST, nc.scalar.copy, slice(1, 2), slice(0, ROWS))
        regroup_relu(LAST, 2)
        regroup_relu(LAST, 3)
        regroup(LAST, nc.vector.tensor_copy, slice(0, 1), slice(0, ROWS))
        quantise_a(LAST, 2, 4)
        quantise_w(LAST, 0)
        quantise_a(LAST, 0, 2)
        quantise_w(LAST, 1)
        multiply(LAST)
        add_bias(LAST)

        last = BLOCKS - 1
        nc.scalar.activation(out=y_sb[:, :last, :], in_=y_sb[:, :last, :], func=ACT.Sigmoid)
        nc.sync.dma_start(out=out[:, :last, :], in_=y_sb[:, :last, :])
        nc.scalar.activation(out=y_sb[:, last, :], in_=y_sb[:, last, :], func=ACT.Sigmoid)
        nc.sync.dma_start(out=out[:, last, :], in_=y_sb[:, last, :])
